import numpy as np
import ml_dtypes


def mxq(x, axis, fmt="e4m3"):
    dtype, down = {"e4m3": (ml_dtypes.float8_e4m3fn, 7), "e5m2": (ml_dtypes.float8_e5m2, 14)}[fmt]
    v = np.moveaxis(np.asarray(x, np.float32).astype(ml_dtypes.bfloat16).astype(np.float64), axis, -1)
    blocks = v.reshape(v.shape[:-1] + (-1, 32))
    amax = np.abs(blocks).max(-1, keepdims=True)
    byte = np.maximum(np.where(amax > 0, np.frexp(amax)[1] - 1 + 127, 0) - down, 1)
    scale = np.exp2(byte - 127.0)
    codes = (blocks / scale).astype(np.float32).astype(dtype).astype(np.float64)
    return np.moveaxis((codes * scale).reshape(v.shape), -1, axis)


WIDE = False


def mx_kscale(k):
    if not WIDE:
        return np.ones(k)
    levels = np.array([10, -10, 5, -5, 0])
    a = np.random.permutation(np.resize(levels, k // 512 * 4)).reshape(k // 512, 4)
    idx = np.arange(k)
    return np.exp2(a[idx // 512, idx % 128 // 32])


BF16 = ml_dtypes.bfloat16


def bf(x):
    return np.asarray(x, np.float32).astype(BF16)


def f64(x):
    return np.asarray(x).astype(np.float64)


E2M1 = np.array([0.0, 0.5, 1.0, 1.5, 2.0, 3.0, 4.0, 6.0, -0.0, -0.5, -1.0, -1.5, -2.0, -3.0, -4.0, -6.0])


def pack_weight(w, fmt):
    k, n = w.shape
    w = f64(bf(w)).reshape(k // 32, 32, n)
    amax = np.abs(w).max(1)
    if fmt == "e4m3":
        byte = np.frexp(amax)[1] - 1 + 127 - 7
    else:
        mant, ex = np.frexp(amax / 6.0)
        byte = np.where(mant > 0.5, ex, ex - 1) + 127
    byte = np.clip(np.where(amax > 0, byte, 1), 1, 254)
    scaled = (w * np.exp2(127.0 - byte)[:, None, :]).reshape(k, n).astype(np.float32)
    by_word = np.ascontiguousarray(scaled.reshape(k // 512, 128, 4, n).transpose(0, 1, 3, 2))
    if fmt == "e4m3":
        words = by_word.astype(ml_dtypes.float8_e4m3fn).view(np.uint8)
    else:
        c = by_word.astype(ml_dtypes.float4_e2m1fn).view(np.uint8) & 0xF
        words = c[..., 0::2] | (c[..., 1::2] << 4)
    return np.ascontiguousarray(words), np.ascontiguousarray(byte.astype(np.uint8).reshape(k // 512, 16, n))


def unpack_weight(words, scales, fmt):
    g, p, n, _ = words.shape
    if fmt == "e4m3":
        vals = np.ascontiguousarray(words).view(ml_dtypes.float8_e4m3fn).astype(np.float64)
    else:
        nib = np.empty((g, p, n, 4), np.uint8)
        nib[..., 0::2] = words & 0xF
        nib[..., 1::2] = words >> 4
        vals = E2M1[nib]
    vals = vals * np.repeat(np.exp2(scales.astype(np.float64) - 127.0), 8, axis=1)[..., None]
    return vals.transpose(0, 1, 3, 2).reshape(g * 512, n)


B, M, N, P = 6, 1024, 1024, 512
EPS = 1e-05


def normalize(v, axes, gamma, beta):
    mean = v.mean(axis=axes, keepdims=True)
    std = np.sqrt(v.var(axis=axes, keepdims=True, ddof=1))
    return gamma * ((v - mean) / (std + EPS)) + beta


def setup_inputs():
    s = mx_kscale(M)
    x = bf(np.random.standard_normal((B, M, N)) * s[:, None])
    xj_words, xj_scales = pack_weight(np.random.standard_normal((M, P)) * 0.5 / np.sqrt(M) / s[:, None], "e4m3")
    xi_words, xi_scales = pack_weight(np.random.standard_normal((N, P)) * 2.0 / np.sqrt(N), "e4m3")
    return {"x": x,
            "permuted_xj_y_words": xj_words,
            "permuted_xj_y_scales": xj_scales,
            "permuted_xi_y_words": xi_words,
            "permuted_xi_y_scales": xi_scales,
            "gamma_p_sum": bf(1.0 + 0.1 * np.random.standard_normal(P)),
            "gamma_p": bf(1.0 + 0.1 * np.random.standard_normal((P, P))),
            "beta_p_sum": bf(0.1 * np.random.standard_normal(P)),
            "beta_p": bf(0.1 * np.random.standard_normal((P, P)))}


def reference(x, permuted_xj_y_words, permuted_xj_y_scales, permuted_xi_y_words, permuted_xi_y_scales, gamma_p_sum, gamma_p, beta_p_sum, beta_p):
    permuted = np.swapaxes(f64(x), -1, -2)
    pyy = mxq(permuted, 2, "e4m3") @ unpack_weight(permuted_xj_y_words, permuted_xj_y_scales, "e4m3")
    p_sum = normalize(pyy.sum(axis=-2), (-1,), f64(gamma_p_sum), f64(beta_p_sum)) + 1.0
    pyy = mxq(np.swapaxes(pyy, -1, -2), 2, "e4m3") @ unpack_weight(permuted_xi_y_words, permuted_xi_y_scales, "e4m3")
    pyy = np.swapaxes(pyy, -1, -2)
    pyy = normalize(pyy, (-2, -1), f64(gamma_p), f64(beta_p))
    return pyy, p_sum

@@ -1,0 +1,303 @@
+from contextlib import ExitStack
+
+import concourse.mybir as mybir
+
+FP8X4 = mybir.dt.float8_e4m3fn_x4
+BF16 = mybir.dt.bfloat16
+F32 = mybir.dt.float32
+U32 = mybir.dt.uint32
+I32 = mybir.dt.int32
+U8 = mybir.dt.uint8
+ACT = mybir.ActivationFunctionType
+ALU = mybir.AluOpType
+AXIS = mybir.AxisListType
+
+BATCH = 6
+M_ROWS = 1024
+N_COLS = 1024
+WIDTH = 512
+EPS = 1e-05
+
+PARTS = 128
+PACK = 4
+K_PASS = PARTS * PACK
+PASSES = M_ROWS // K_PASS
+TILES = WIDTH // PARTS
+SCALE_ROWS = K_PASS // 32
+UNITS = PASSES * TILES
+VECTOR_SHARE = 96
+
+FLOPS = 2 * BATCH * (M_ROWS * N_COLS * WIDTH + N_COLS * WIDTH * WIDTH)
+
+
+def live(b):
+    return 0 <= b < BATCH
+
+
+def load_weight(nc, keep, words, scales, label):
+    codes = keep.tile([PARTS, PASSES, WIDTH], U32, name=label + "_codes", align_bytes=64)
+    planes = keep.tile([PARTS, PASSES, WIDTH], U8, name=label + "_planes", align_bytes=64)
+    nc.vector.memset(planes[:].bitcast(I32), 0)
+    nc.sync.dma_start(out=codes[:].bitcast(I32), in_=words.rearrange("g p n t -> p g (n t)").bitcast(I32))
+    for r in range(PACK):
+        nc.sync.dma_start(
+            out=planes[r:PARTS:32, :, :].bitcast(I32),
+            in_=scales[:, r:SCALE_ROWS:PACK, :].rearrange("g q n -> q g n").bitcast(I32),
+        )
+    return codes, planes
+
+
+def tile_selfprojection_pb_kernel(
+    tc,
+    x,
+    permuted_xj_y_words,
+    permuted_xj_y_scales,
+    permuted_xi_y_words,
+    permuted_xi_y_scales,
+    gamma_p_sum,
+    gamma_p,
+    beta_p_sum,
+    beta_p,
+    out_0,
+    out_1,
+):
+    nc = tc.nc
+    with ExitStack() as ctx:
+        keep = ctx.enter_context(tc.tile_pool(name="keep", bufs=1))
+        raw_pool = ctx.enter_context(tc.tile_pool(name="raw", bufs=2 * PASSES * PASSES))
+        grouped_pool = ctx.enter_context(tc.tile_pool(name="grouped", bufs=4))
+        x_pool = ctx.enter_context(tc.tile_pool(name="xq", bufs=2))
+        y_pool = ctx.enter_context(tc.tile_pool(name="yq", bufs=2))
+        z_pool = ctx.enter_context(tc.tile_pool(name="z", bufs=2))
+        small = ctx.enter_context(tc.tile_pool(name="small", bufs=3))
+        psum_y = ctx.enter_context(tc.psum_pool(name="psum_y", bufs=3))
+        psum_c = ctx.enter_context(tc.psum_pool(name="psum_c", bufs=1))
+        psum_z = ctx.enter_context(tc.psum_pool(name="psum_z", bufs=2))
+        psum_s = ctx.enter_context(tc.psum_pool(name="psum_s", bufs=1))
+        psum_p = ctx.enter_context(tc.psum_pool(name="psum_p", bufs=1))
+        held = {}
+
+        def load_x(b, gn):
+            for gm in range(PASSES):
+                piece = raw_pool.tile([PARTS, PACK, K_PASS], BF16, name="raw_piece")
+                nc.sync.dma_start(
+                    out=piece[:],
+                    in_=x[b, K_PASS * gm : K_PASS * (gm + 1), K_PASS * gn : K_PASS * (gn + 1)].rearrange(
+                        "(p t) n -> p t n", t=PACK
+                    ),
+                )
+                held[("raw", b, PASSES * gn + gm)] = piece
+
+        def regroup_x(b, piece):
+            if piece == 0:
+                held[("x_codes", b)] = x_pool.tile([PARTS, PASSES, N_COLS], U32, name="x_codes", align_bytes=64)
+                held[("x_planes", b)] = x_pool.tile([PARTS, PASSES, N_COLS], U8, name="x_planes", align_bytes=64)
+            grouped = grouped_pool.tile([PARTS, PACK, PARTS, PACK], BF16, name="grouped", align_bytes=64)
+            source = held[("raw", b, piece)][:].rearrange("p tm (q tn) -> p tn q tm", tn=PACK)
+            nc.vector.tensor_copy(out=grouped[:, :, :VECTOR_SHARE, :], in_=source[:, :, :VECTOR_SHARE, :])
+            nc.scalar.copy(out=grouped[:, :, VECTOR_SHARE:, :], in_=source[:, :, VECTOR_SHARE:, :])
+            held[("grouped", b, piece)] = grouped
+
+        def quantise_x(b, piece):
+            gn, gm = divmod(piece, PASSES)
+            cols = slice(K_PASS * gn, K_PASS * (gn + 1))
+            nc.vector.quantize_mx(
+                out=held[("x_codes", b)][:, gm, cols].bitcast(FP8X4),
+                scales=held[("x_planes", b)][:, gm, cols],
+                in_=held[("grouped", b, piece)][:].rearrange("p tn q tm -> p (tn q tm)"),
+            )
+
+        def first_product_unit(b, unit):
+            gn, jt = divmod(unit, TILES)
+            x_codes = held[("x_codes", b)]
+            x_planes = held[("x_planes", b)]
+            if unit == 0:
+                held[("y_grouped", b)] = y_pool.tile([PARTS, PASSES, WIDTH, PACK], BF16, name="y_grouped", align_bytes=64)
+                held[("c_bank", b)] = psum_c.tile([PARTS, WIDTH], F32, name="c_bank")
+            c_bank = held[("c_bank", b)]
+            n_cols = slice(PARTS * unit, PARTS * (unit + 1))
+            for gm in range(PASSES):
+                nc.tensor.matmul_mx(
+                    out=c_bank[:],
+                    lhsT=x_codes[:, gm, n_cols].bitcast(FP8X4),
+                    lhsT_scale=x_planes[:, gm, n_cols],
+                    rhs=wj_codes[:, gm, :].bitcast(FP8X4),
+                    rhs_scale=wj_planes[:, gm, :],
+                    start=(unit == 0 and gm == 0),
+                    stop=(unit == UNITS - 1 and gm == PASSES - 1),
+                )
+            if unit == UNITS - 1:
+                c_parts = small.tile([PARTS, WIDTH], F32, name="c_parts")
+                nc.scalar.copy(out=c_parts[:], in_=c_bank[:])
+                held[("c_parts", b)] = c_parts
+            j_cols = slice(PARTS * jt, PARTS * (jt + 1))
+            y_bank = psum_y.tile([PARTS, PACK, PARTS], F32, name="y_bank")
+            for tn in range(PACK):
+                n_cols = slice(K_PASS * gn + PARTS * tn, K_PASS * gn + PARTS * (tn + 1))
+                for gm in range(PASSES):
+                    nc.tensor.matmul_mx(
+                        out=y_bank[:, tn, :],
+                        lhsT=x_codes[:, gm, n_cols].bitcast(FP8X4),
+                        lhsT_scale=x_planes[:, gm, n_cols],
+                        rhs=wj_codes[:, gm, j_cols].bitcast(FP8X4),
+                        rhs_scale=wj_planes[:, gm, j_cols],
+                        start=(gm == 0),
+                        stop=(gm == PASSES - 1),
+                    )
+            nc.scalar.copy(out=held[("y_grouped", b)][:, gn, j_cols, :], in_=y_bank[:].rearrange("p t j -> p j t"))
+
+        def quantise_y(b, gn):
+            if gn == 0:
+                held[("y_codes", b)] = y_pool.tile([PARTS, PASSES, WIDTH], U32, name="y_codes", align_bytes=64)
+                held[("y_planes", b)] = y_pool.tile([PARTS, PASSES, WIDTH], U8, name="y_planes", align_bytes=64)
+            nc.vector.quantize_mx(
+                out=held[("y_codes", b)][:, gn, :].bitcast(FP8X4),
+                scales=held[("y_planes", b)][:, gn, :],
+                in_=held[("y_grouped", b)][:, gn, :, :].rearrange("p j t -> p (j t)"),
+            )
+
+        def collect_column_sum(b):
+            nc.tensor.matmul(
+                out=c_all[:], lhsT=pick[:, b, :], rhs=held[("c_parts", b)][:], start=(b == 0), stop=(b == BATCH - 1)
+            )
+
+        def second_product(b):
+            z_sb = z_pool.tile([PARTS, TILES, WIDTH], F32, name="z_sb")
+            z_sum = small.tile([PARTS, TILES], F32, name="z_sum")
+            for it in range(TILES):
+                i_cols = slice(PARTS * it, PARTS * (it + 1))
+                z_bank = psum_z.tile([PARTS, WIDTH], F32, name="z_bank")
+                for gn in range(PASSES):
+                    nc.tensor.matmul_mx(
+                        out=z_bank[:],
+                        lhsT=wi_codes[:, gn, i_cols].bitcast(FP8X4),
+                        lhsT_scale=wi_planes[:, gn, i_cols],
+                        rhs=held[("y_codes", b)][:, gn, :].bitcast(FP8X4),
+                        rhs_scale=held[("y_planes", b)][:, gn, :],
+                        start=(gn == 0),
+                        stop=(gn == PASSES - 1),
+                    )
+                nc.scalar.activation(out=z_sb[:, it, :], in_=z_bank[:], func=ACT.Copy, accum_out=z_sum[:, it : it + 1])
+            held[("z_sb", b)] = z_sb
+            held[("z_sum", b)] = z_sum
+
+        def mean(b):
+            mean_ps = psum_s.tile([PARTS, TILES], F32, name="mean_ps", tag="stat")
+            nc.tensor.matmul(out=mean_ps[:], lhsT=neg_share[:], rhs=held[("z_sum", b)][:], start=True, stop=True)
+            neg_mean = small.tile([PARTS, 1], F32, name="neg_mean")
+            nc.vector.tensor_reduce(out=neg_mean[:], in_=mean_ps[:], axis=AXIS.X, op=ALU.add)
+            held[("neg_mean", b)] = neg_mean
+            held[("dev_sq", b)] = small.tile([PARTS, TILES], F32, name="dev_sq")
+            held[("scaled", b)] = z_pool.tile([PARTS, TILES, WIDTH], F32, name="scaled")
+
+        def deviations(b, it):
+            z_tile = held[("z_sb", b)][:, it, :]
+            neg_mean = held[("neg_mean", b)]
+            squares = small.tile([PARTS, WIDTH], BF16, name="squares")
+            nc.scalar.activation(
+                out=squares[:], in_=z_tile, func=ACT.Square, bias=neg_mean[:], accum_out=held[("dev_sq", b)][:, it : it + 1]
+            )
+            nc.vector.scalar_tensor_tensor(
+                out=held[("scaled", b)][:, it, :], in0=z_tile, scalar=neg_mean[:], in1=gamma_sb[:, it, :], op0=ALU.add, op1=ALU.mult
+            )
+
+        def spread_begin(b):
+            ssq_ps = psum_s.tile([PARTS, TILES], F32, name="ssq_ps", tag="stat")
+            nc.tensor.matmul(out=ssq_ps[:], lhsT=ones[:], rhs=held[("dev_sq", b)][:], start=True, stop=True)
+            ssq = small.tile([PARTS, 1], F32, name="ssq")
+            nc.vector.tensor_reduce(out=ssq[:], in_=ssq_ps[:], axis=AXIS.X, op=ALU.add)
+            std = small.tile([PARTS, 1], F32, name="std")
+            nc.scalar.activation(out=std[:], in_=ssq[:], func=ACT.Sqrt, scale=1.0 / (WIDTH * WIDTH - 1))
+            held[("std", b)] = std
+
+        def spread_end(b):
+            inv_std = small.tile([PARTS, 1], F32, name="inv_std")
+            nc.vector.tensor_scalar_add(out=inv_std[:], in0=held[("std", b)][:], scalar1=EPS)
+            nc.vector.reciprocal(out=inv_std[:], in_=inv_std[:])
+            held[("inv_std", b)] = inv_std
+
+        def finish(b, it):
+            tile_out = held[("scaled", b)][:, it, :]
+            nc.vector.scalar_tensor_tensor(
+                out=tile_out, in0=tile_out, scalar=held[("inv_std", b)][:], in1=beta_sb[:, it, :], op0=ALU.mult, op1=ALU.add
+            )
+            nc.sync.dma_start(out=out_0[b, PARTS * it : PARTS * (it + 1), :], in_=tile_out)
+
+        def normalise_column_sums():
+            c_stats = small.tile([BATCH, 6], F32, name="c_stats")
+            nc.vector.bn_stats(out=c_stats[:], in_=c_all[:BATCH, :])
+            c_mv = small.tile([BATCH, 2], F32, name="c_mv")
+            nc.vector.bn_aggr(out=c_mv[:], in_=c_stats[:])
+            c_std = small.tile([BATCH, 1], F32, name="c_std")
+            nc.scalar.activation(out=c_std[:], in_=c_mv[:, 1:2], func=ACT.Sqrt, scale=WIDTH / (WIDTH - 1.0))
+            c_inv = small.tile([BATCH, 1], F32, name="c_inv")
+            nc.vector.tensor_scalar_add(out=c_inv[:], in0=c_std[:], scalar1=EPS)
+            nc.vector.reciprocal(out=c_inv[:], in_=c_inv[:])
+            p_sum = small.tile([BATCH, WIDTH], F32, name="p_sum")
+            nc.vector.tensor_scalar(
+                out=p_sum[:], in0=c_all[:BATCH, :], scalar1=c_mv[:, 0:1], scalar2=c_inv[:], op0=ALU.subtract, op1=ALU.mult
+            )
+            nc.vector.tensor_mul(out=p_sum[:], in0=p_sum[:], in1=gain_c[:])
+            nc.vector.scalar_tensor_tensor(out=p_sum[:], in0=p_sum[:], scalar=1.0, in1=bias_c[:], op0=ALU.add, op1=ALU.add)
+            nc.sync.dma_start(out=out_1[:, :], in_=p_sum[:])
+
+        warm = keep.tile([PARTS, 1], F32, name="warm")
+        nc.vector.memset(warm[:], 1.0)
+        nc.scalar.activation(out=warm[:], in_=warm[:], func=ACT.Sqrt)
+
+        load_x(0, 0)
+        wj_codes, wj_planes = load_weight(nc, keep, permuted_xj_y_words, permuted_xj_y_scales, "wj")
+        load_x(0, 1)
+        wi_codes, wi_planes = load_weight(nc, keep, permuted_xi_y_words, permuted_xi_y_scales, "wi")
+        load_x(1, 0)
+        load_x(1, 1)
+        gamma_sb = keep.tile([PARTS, TILES, WIDTH], BF16, name="gamma_sb")
+        beta_sb = keep.tile([PARTS, TILES, WIDTH], BF16, name="beta_sb")
+        nc.sync.dma_start(out=gamma_sb[:], in_=gamma_p.rearrange("(t p) j -> p t j", p=PARTS))
+        nc.sync.dma_start(out=beta_sb[:], in_=beta_p.rearrange("(t p) j -> p t j", p=PARTS))
+        gain_c = keep.tile([BATCH, WIDTH], BF16, name="gain_c")
+        bias_c = keep.tile([BATCH, WIDTH], BF16, name="bias_c")
+        nc.sync.dma_start(out=gain_c[:], in_=gamma_p_sum.partition_broadcast(BATCH))
+        nc.sync.dma_start(out=bias_c[:], in_=beta_p_sum.partition_broadcast(BATCH))
+
+        ones = keep.tile([PARTS, PARTS], F32, name="ones")
+        nc.gpsimd.memset(ones[:], 1.0)
+        neg_share = keep.tile([PARTS, PARTS], F32, name="neg_share")
+        nc.gpsimd.memset(neg_share[:], -1.0 / (WIDTH * WIDTH))
+        pick = keep.tile([PARTS, BATCH, PARTS], F32, name="pick")
+        nc.gpsimd.memset(pick[:], 0.0)
+        for b in range(BATCH):
+            nc.gpsimd.memset(pick[:, b, b : b + 1], 1.0)
+        c_all = psum_p.tile([PARTS, WIDTH], F32, name="c_all")
+
+        for r in range(-1, BATCH + 2):
+            if r >= 0 and live(r + 2):
+                load_x(r + 2, 0)
+                load_x(r + 2, 1)
+            for unit in range(UNITS):
+                if live(r + 1):
+                    if unit % 2 == 0:
+                        regroup_x(r + 1, unit // 2)
+                    else:
+                        quantise_x(r + 1, unit // 2)
+                if live(r):
+                    first_product_unit(r, unit)
+                if live(r - 1) and unit == 1:
+                    collect_column_sum(r - 1)
+                    second_product(r - 1)
+                    if r - 1 == BATCH - 1:
+                        normalise_column_sums()
+                if live(r - 2):
+                    if unit == 1:
+                        spread_begin(r - 2)
+                    if unit == 2:
+                        spread_end(r - 2)
+                    if 2 <= unit < 2 + TILES:
+                        finish(r - 2, unit - 2)
+                if live(r - 1):
+                    if unit == TILES - 1:
+                        mean(r - 1)
+                    if unit >= TILES:
+                        deviations(r - 1, unit - TILES)
+                if live(r) and unit % TILES == TILES - 1:
+                    quantise_y(r, unit // TILES)

@@ -93,9 +93,10 @@ def tile_selfprojection_pb_kernel(
                 held[("x_codes", b)] = x_pool.tile([PARTS, PASSES, N_COLS], U32, name="x_codes", align_bytes=64)
                 held[("x_planes", b)] = x_pool.tile([PARTS, PASSES, N_COLS], U8, name="x_planes", align_bytes=64)
             grouped = grouped_pool.tile([PARTS, PACK, PARTS, PACK], BF16, name="grouped", align_bytes=64)
-            source = held[("raw", b, piece)][:].rearrange("p tm (q tn) -> p tn q tm", tn=PACK)
-            nc.vector.tensor_copy(out=grouped[:, :, :VECTOR_SHARE, :], in_=source[:, :, :VECTOR_SHARE, :])
-            nc.scalar.copy(out=grouped[:, :, VECTOR_SHARE:, :], in_=source[:, :, VECTOR_SHARE:, :])
+            source = held[("raw", b, piece)][:].rearrange("p tm (q tn) -> p q tm tn", tn=PACK)
+            target = grouped[:].rearrange("p tn q tm -> p q tm tn")
+            nc.vector.tensor_copy(out=target[:, :VECTOR_SHARE, :, :], in_=source[:, :VECTOR_SHARE, :, :])
+            nc.scalar.copy(out=target[:, VECTOR_SHARE:, :, :], in_=source[:, VECTOR_SHARE:, :, :])
             held[("grouped", b, piece)] = grouped
 
         def quantise_x(b, piece):

@@ -10,7 +10,6 @@ I32 = mybir.dt.int32
 U8 = mybir.dt.uint8
 ACT = mybir.ActivationFunctionType
 ALU = mybir.AluOpType
-AXIS = mybir.AxisListType
 
 BATCH = 6
 M_ROWS = 1024
@@ -68,12 +67,11 @@ def tile_selfprojection_pb_kernel(
         grouped_pool = ctx.enter_context(tc.tile_pool(name="grouped", bufs=4))
         x_pool = ctx.enter_context(tc.tile_pool(name="xq", bufs=2))
         y_pool = ctx.enter_context(tc.tile_pool(name="yq", bufs=2))
-        z_pool = ctx.enter_context(tc.tile_pool(name="z", bufs=2))
+        z_pool = ctx.enter_context(tc.tile_pool(name="z", bufs=3))
         small = ctx.enter_context(tc.tile_pool(name="small", bufs=3))
         psum_y = ctx.enter_context(tc.psum_pool(name="psum_y", bufs=3))
-        psum_c = ctx.enter_context(tc.psum_pool(name="psum_c", bufs=1))
+        psum_c = ctx.enter_context(tc.psum_pool(name="psum_c", bufs=2))
         psum_z = ctx.enter_context(tc.psum_pool(name="psum_z", bufs=2))
-        psum_s = ctx.enter_context(tc.psum_pool(name="psum_s", bufs=1))
         psum_p = ctx.enter_context(tc.psum_pool(name="psum_p", bufs=1))
         held = {}
 
@@ -162,31 +160,32 @@ def tile_selfprojection_pb_kernel(
                 out=c_all[:], lhsT=pick[:, b, :], rhs=held[("c_parts", b)][:], start=(b == 0), stop=(b == BATCH - 1)
             )
 
-        def second_product(b):
-            z_sb = z_pool.tile([PARTS, TILES, WIDTH], F32, name="z_sb")
-            z_sum = small.tile([PARTS, TILES], F32, name="z_sum")
-            for it in range(TILES):
-                i_cols = slice(PARTS * it, PARTS * (it + 1))
-                z_bank = psum_z.tile([PARTS, WIDTH], F32, name="z_bank")
-                for gn in range(PASSES):
-                    nc.tensor.matmul_mx(
-                        out=z_bank[:],
-                        lhsT=wi_codes[:, gn, i_cols].bitcast(FP8X4),
-                        lhsT_scale=wi_planes[:, gn, i_cols],
-                        rhs=held[("y_codes", b)][:, gn, :].bitcast(FP8X4),
-                        rhs_scale=held[("y_planes", b)][:, gn, :],
-                        start=(gn == 0),
-                        stop=(gn == PASSES - 1),
-                    )
-                nc.scalar.activation(out=z_sb[:, it, :], in_=z_bank[:], func=ACT.Copy, accum_out=z_sum[:, it : it + 1])
-            held[("z_sb", b)] = z_sb
-            held[("z_sum", b)] = z_sum
+        def second_product_tile(b, it):
+            if it == 0:
+                held[("z_sb", b)] = z_pool.tile([PARTS, TILES, WIDTH], F32, name="z_sb")
+                held[("z_sum", b)] = small.tile([PARTS, TILES], F32, name="z_sum")
+            i_cols = slice(PARTS * it, PARTS * (it + 1))
+            z_bank = psum_z.tile([PARTS, WIDTH], F32, name="z_bank")
+            for gn in range(PASSES):
+                nc.tensor.matmul_mx(
+                    out=z_bank[:],
+                    lhsT=wi_codes[:, gn, i_cols].bitcast(FP8X4),
+                    lhsT_scale=wi_planes[:, gn, i_cols],
+                    rhs=held[("y_codes", b)][:, gn, :].bitcast(FP8X4),
+                    rhs_scale=held[("y_planes", b)][:, gn, :],
+                    start=(gn == 0),
+                    stop=(gn == PASSES - 1),
+                )
+            nc.scalar.activation(
+                out=held[("z_sb", b)][:, it, :], in_=z_bank[:], func=ACT.Copy, accum_out=held[("z_sum", b)][:, it : it + 1]
+            )
 
         def mean(b):
-            mean_ps = psum_s.tile([PARTS, TILES], F32, name="mean_ps", tag="stat")
+            mean_ps = psum_z.tile([PARTS, TILES], F32, name="mean_ps", tag="z_bank")
             nc.tensor.matmul(out=mean_ps[:], lhsT=neg_share[:], rhs=held[("z_sum", b)][:], start=True, stop=True)
             neg_mean = small.tile([PARTS, 1], F32, name="neg_mean")
-            nc.vector.tensor_reduce(out=neg_mean[:], in_=mean_ps[:], axis=AXIS.X, op=ALU.add)
+            spare = small.tile([PARTS, TILES], F32, name="spare")
+            nc.scalar.activation(out=spare[:], in_=mean_ps[:], func=ACT.Copy, accum_out=neg_mean[:])
             held[("neg_mean", b)] = neg_mean
             held[("dev_sq", b)] = small.tile([PARTS, TILES], F32, name="dev_sq")
             held[("scaled", b)] = z_pool.tile([PARTS, TILES, WIDTH], F32, name="scaled")
@@ -203,10 +202,11 @@ def tile_selfprojection_pb_kernel(
             )
 
         def spread_begin(b):
-            ssq_ps = psum_s.tile([PARTS, TILES], F32, name="ssq_ps", tag="stat")
+            ssq_ps = psum_z.tile([PARTS, TILES], F32, name="ssq_ps", tag="z_bank")
             nc.tensor.matmul(out=ssq_ps[:], lhsT=ones[:], rhs=held[("dev_sq", b)][:], start=True, stop=True)
             ssq = small.tile([PARTS, 1], F32, name="ssq")
-            nc.vector.tensor_reduce(out=ssq[:], in_=ssq_ps[:], axis=AXIS.X, op=ALU.add)
+            spare = small.tile([PARTS, TILES], F32, name="spare")
+            nc.scalar.activation(out=spare[:], in_=ssq_ps[:], func=ACT.Copy, accum_out=ssq[:])
             std = small.tile([PARTS, 1], F32, name="std")
             nc.scalar.activation(out=std[:], in_=ssq[:], func=ACT.Sqrt, scale=1.0 / (WIDTH * WIDTH - 1))
             held[("std", b)] = std
@@ -283,11 +283,18 @@ def tile_selfprojection_pb_kernel(
                         quantise_x(r + 1, unit // 2)
                 if live(r):
                     first_product_unit(r, unit)
-                if live(r - 1) and unit == 1:
-                    collect_column_sum(r - 1)
-                    second_product(r - 1)
-                    if r - 1 == BATCH - 1:
-                        normalise_column_sums()
+                if live(r - 1):
+                    if unit == 1:
+                        collect_column_sum(r - 1)
+                        if r - 1 == BATCH - 1:
+                            normalise_column_sums()
+                    if 2 <= unit < 2 + TILES:
+                        second_product_tile(r - 1, unit - 2)
+                    if unit == 2 + TILES:
+                        mean(r - 1)
+                    if unit == 3 + TILES:
+                        for it in range(TILES):
+                            deviations(r - 1, it)
                 if live(r - 2):
                     if unit == 1:
                         spread_begin(r - 2)
@@ -295,10 +302,5 @@ def tile_selfprojection_pb_kernel(
                         spread_end(r - 2)
                     if 2 <= unit < 2 + TILES:
                         finish(r - 2, unit - 2)
-                if live(r - 1):
-                    if unit == TILES - 1:
-                        mean(r - 1)
-                    if unit >= TILES:
-                        deviations(r - 1, unit - TILES)
                 if live(r) and unit % TILES == TILES - 1:
                     quantise_y(r, unit // TILES)

@@ -10,6 +10,7 @@ I32 = mybir.dt.int32
 U8 = mybir.dt.uint8
 ACT = mybir.ActivationFunctionType
 ALU = mybir.AluOpType
+AXIS = mybir.AxisListType
 
 BATCH = 6
 M_ROWS = 1024
@@ -24,7 +25,7 @@ PASSES = M_ROWS // K_PASS
 TILES = WIDTH // PARTS
 SCALE_ROWS = K_PASS // 32
 UNITS = PASSES * TILES
-VECTOR_SHARE = 96
+VECTOR_SHARE = 112
 
 FLOPS = 2 * BATCH * (M_ROWS * N_COLS * WIDTH + N_COLS * WIDTH * WIDTH)
 
@@ -67,11 +68,12 @@ def tile_selfprojection_pb_kernel(
         grouped_pool = ctx.enter_context(tc.tile_pool(name="grouped", bufs=4))
         x_pool = ctx.enter_context(tc.tile_pool(name="xq", bufs=2))
         y_pool = ctx.enter_context(tc.tile_pool(name="yq", bufs=2))
-        z_pool = ctx.enter_context(tc.tile_pool(name="z", bufs=3))
+        z_pool = ctx.enter_context(tc.tile_pool(name="z", bufs=2))
         small = ctx.enter_context(tc.tile_pool(name="small", bufs=3))
         psum_y = ctx.enter_context(tc.psum_pool(name="psum_y", bufs=3))
-        psum_c = ctx.enter_context(tc.psum_pool(name="psum_c", bufs=2))
+        psum_c = ctx.enter_context(tc.psum_pool(name="psum_c", bufs=1))
         psum_z = ctx.enter_context(tc.psum_pool(name="psum_z", bufs=2))
+        psum_s = ctx.enter_context(tc.psum_pool(name="psum_s", bufs=1))
         psum_p = ctx.enter_context(tc.psum_pool(name="psum_p", bufs=1))
         held = {}
 
@@ -160,55 +162,54 @@ def tile_selfprojection_pb_kernel(
                 out=c_all[:], lhsT=pick[:, b, :], rhs=held[("c_parts", b)][:], start=(b == 0), stop=(b == BATCH - 1)
             )
 
-        def second_product_tile(b, it):
-            if it == 0:
-                held[("z_sb", b)] = z_pool.tile([PARTS, TILES, WIDTH], F32, name="z_sb")
-                held[("z_sum", b)] = small.tile([PARTS, TILES], F32, name="z_sum")
-            i_cols = slice(PARTS * it, PARTS * (it + 1))
-            z_bank = psum_z.tile([PARTS, WIDTH], F32, name="z_bank")
-            for gn in range(PASSES):
-                nc.tensor.matmul_mx(
-                    out=z_bank[:],
-                    lhsT=wi_codes[:, gn, i_cols].bitcast(FP8X4),
-                    lhsT_scale=wi_planes[:, gn, i_cols],
-                    rhs=held[("y_codes", b)][:, gn, :].bitcast(FP8X4),
-                    rhs_scale=held[("y_planes", b)][:, gn, :],
-                    start=(gn == 0),
-                    stop=(gn == PASSES - 1),
-                )
-            nc.scalar.activation(
-                out=held[("z_sb", b)][:, it, :], in_=z_bank[:], func=ACT.Copy, accum_out=held[("z_sum", b)][:, it : it + 1]
-            )
+        def second_product(b):
+            z_sb = z_pool.tile([PARTS, TILES, WIDTH], F32, name="z_sb")
+            z_sum = small.tile([PARTS, TILES], F32, name="z_sum")
+            for it in range(TILES):
+                i_cols = slice(PARTS * it, PARTS * (it + 1))
+                z_bank = psum_z.tile([PARTS, WIDTH], F32, name="z_bank")
+                for gn in range(PASSES):
+                    nc.tensor.matmul_mx(
+                        out=z_bank[:],
+                        lhsT=wi_codes[:, gn, i_cols].bitcast(FP8X4),
+                        lhsT_scale=wi_planes[:, gn, i_cols],
+                        rhs=held[("y_codes", b)][:, gn, :].bitcast(FP8X4),
+                        rhs_scale=held[("y_planes", b)][:, gn, :],
+                        start=(gn == 0),
+                        stop=(gn == PASSES - 1),
+                    )
+                nc.scalar.activation(out=z_sb[:, it, :], in_=z_bank[:], func=ACT.Copy, accum_out=z_sum[:, it : it + 1])
+            held[("z_sb", b)] = z_sb
+            held[("z_sum", b)] = z_sum
 
         def mean(b):
-            mean_ps = psum_z.tile([PARTS, TILES], F32, name="mean_ps", tag="z_bank")
+            mean_ps = psum_s.tile([PARTS, TILES], F32, name="mean_ps", tag="stat")
             nc.tensor.matmul(out=mean_ps[:], lhsT=neg_share[:], rhs=held[("z_sum", b)][:], start=True, stop=True)
             neg_mean = small.tile([PARTS, 1], F32, name="neg_mean")
-            spare = small.tile([PARTS, TILES], F32, name="spare")
-            nc.scalar.activation(out=spare[:], in_=mean_ps[:], func=ACT.Copy, accum_out=neg_mean[:])
+            nc.vector.tensor_reduce(out=neg_mean[:], in_=mean_ps[:], axis=AXIS.X, op=ALU.add)
             held[("neg_mean", b)] = neg_mean
-            held[("dev_sq", b)] = small.tile([PARTS, TILES], F32, name="dev_sq")
+            held[("dev_sq", b)] = small.tile([PARTS, 1], F32, name="dev_sq")
             held[("scaled", b)] = z_pool.tile([PARTS, TILES, WIDTH], F32, name="scaled")
 
-        def deviations(b, it):
-            z_tile = held[("z_sb", b)][:, it, :]
+        def deviations(b):
+            z_all = held[("z_sb", b)][:].rearrange("p t j -> p (t j)")
             neg_mean = held[("neg_mean", b)]
-            squares = small.tile([PARTS, WIDTH], BF16, name="squares")
-            nc.scalar.activation(
-                out=squares[:], in_=z_tile, func=ACT.Square, bias=neg_mean[:], accum_out=held[("dev_sq", b)][:, it : it + 1]
-            )
+            squares = z_pool.tile([PARTS, TILES * WIDTH], BF16, name="squares")
+            nc.scalar.activation(out=squares[:], in_=z_all, func=ACT.Square, bias=neg_mean[:], accum_out=held[("dev_sq", b)][:])
             nc.vector.scalar_tensor_tensor(
-                out=held[("scaled", b)][:, it, :], in0=z_tile, scalar=neg_mean[:], in1=gamma_sb[:, it, :], op0=ALU.add, op1=ALU.mult
+                out=held[("scaled", b)][:].rearrange("p t j -> p (t j)"),
+                in0=z_all,
+                scalar=neg_mean[:],
+                in1=gamma_sb[:].rearrange("p t j -> p (t j)"),
+                op0=ALU.add,
+                op1=ALU.mult,
             )
 
         def spread_begin(b):
-            ssq_ps = psum_z.tile([PARTS, TILES], F32, name="ssq_ps", tag="z_bank")
+            ssq_ps = psum_s.tile([PARTS, 1], F32, name="ssq_ps", tag="stat")
             nc.tensor.matmul(out=ssq_ps[:], lhsT=ones[:], rhs=held[("dev_sq", b)][:], start=True, stop=True)
-            ssq = small.tile([PARTS, 1], F32, name="ssq")
-            spare = small.tile([PARTS, TILES], F32, name="spare")
-            nc.scalar.activation(out=spare[:], in_=ssq_ps[:], func=ACT.Copy, accum_out=ssq[:])
             std = small.tile([PARTS, 1], F32, name="std")
-            nc.scalar.activation(out=std[:], in_=ssq[:], func=ACT.Sqrt, scale=1.0 / (WIDTH * WIDTH - 1))
+            nc.scalar.activation(out=std[:], in_=ssq_ps[:], func=ACT.Sqrt, scale=1.0 / (WIDTH * WIDTH - 1))
             held[("std", b)] = std
 
         def spread_end(b):
@@ -283,18 +284,11 @@ def tile_selfprojection_pb_kernel(
                         quantise_x(r + 1, unit // 2)
                 if live(r):
                     first_product_unit(r, unit)
-                if live(r - 1):
-                    if unit == 1:
-                        collect_column_sum(r - 1)
-                        if r - 1 == BATCH - 1:
-                            normalise_column_sums()
-                    if 2 <= unit < 2 + TILES:
-                        second_product_tile(r - 1, unit - 2)
-                    if unit == 2 + TILES:
-                        mean(r - 1)
-                    if unit == 3 + TILES:
-                        for it in range(TILES):
-                            deviations(r - 1, it)
+                if live(r - 1) and unit == 1:
+                    collect_column_sum(r - 1)
+                    second_product(r - 1)
+                    if r - 1 == BATCH - 1:
+                        normalise_column_sums()
                 if live(r - 2):
                     if unit == 1:
                         spread_begin(r - 2)
@@ -302,5 +296,10 @@ def tile_selfprojection_pb_kernel(
                         spread_end(r - 2)
                     if 2 <= unit < 2 + TILES:
                         finish(r - 2, unit - 2)
+                if live(r - 1):
+                    if unit == TILES - 1:
+                        mean(r - 1)
+                    if unit == TILES:
+                        deviations(r - 1)
                 if live(r) and unit % TILES == TILES - 1:
                     quantise_y(r, unit // TILES)

@@ -1,6 +1,7 @@
 from contextlib import ExitStack
 
 import concourse.mybir as mybir
+from concourse.masks import make_identity
 
 FP8X4 = mybir.dt.float8_e4m3fn_x4
 BF16 = mybir.dt.bfloat16
@@ -25,13 +26,12 @@ PASSES = M_ROWS // K_PASS
 TILES = WIDTH // PARTS
 SCALE_ROWS = K_PASS // 32
 UNITS = PASSES * TILES
-VECTOR_SHARE = 112
+PIECES = PASSES * PASSES
+C_WINDOW = 256
+HALVES = 2
+FIRST_SHARE = 88
 
 FLOPS = 2 * BATCH * (M_ROWS * N_COLS * WIDTH + N_COLS * WIDTH * WIDTH)
-
-
-def live(b):
-    return 0 <= b < BATCH
 
 
 def load_weight(nc, keep, words, scales, label):
@@ -64,17 +64,17 @@ def tile_selfprojection_pb_kernel(
     nc = tc.nc
     with ExitStack() as ctx:
         keep = ctx.enter_context(tc.tile_pool(name="keep", bufs=1))
-        raw_pool = ctx.enter_context(tc.tile_pool(name="raw", bufs=2 * PASSES * PASSES))
-        grouped_pool = ctx.enter_context(tc.tile_pool(name="grouped", bufs=4))
-        x_pool = ctx.enter_context(tc.tile_pool(name="xq", bufs=2))
+        raw_pool = ctx.enter_context(tc.tile_pool(name="raw", bufs=3 * PIECES))
+        grouped_pool = ctx.enter_context(tc.tile_pool(name="grouped", bufs=3))
+        x_pool = ctx.enter_context(tc.tile_pool(name="xq", bufs=3))
         y_pool = ctx.enter_context(tc.tile_pool(name="yq", bufs=2))
-        z_pool = ctx.enter_context(tc.tile_pool(name="z", bufs=2))
-        small = ctx.enter_context(tc.tile_pool(name="small", bufs=3))
+        z_pool = ctx.enter_context(tc.tile_pool(name="z", bufs=3))
+        s_pool = ctx.enter_context(tc.tile_pool(name="s", bufs=2))
+        small = ctx.enter_context(tc.tile_pool(name="small", bufs=4))
         psum_y = ctx.enter_context(tc.psum_pool(name="psum_y", bufs=3))
-        psum_c = ctx.enter_context(tc.psum_pool(name="psum_c", bufs=1))
+        psum_c = ctx.enter_context(tc.psum_pool(name="psum_c", bufs=2))
         psum_z = ctx.enter_context(tc.psum_pool(name="psum_z", bufs=2))
         psum_s = ctx.enter_context(tc.psum_pool(name="psum_s", bufs=1))
-        psum_p = ctx.enter_context(tc.psum_pool(name="psum_p", bufs=1))
         held = {}
 
         def load_x(b, gn):
@@ -95,8 +95,10 @@ def tile_selfprojection_pb_kernel(
             grouped = grouped_pool.tile([PARTS, PACK, PARTS, PACK], BF16, name="grouped", align_bytes=64)
             source = held[("raw", b, piece)][:].rearrange("p tm (q tn) -> p q tm tn", tn=PACK)
             target = grouped[:].rearrange("p tn q tm -> p q tm tn")
-            nc.vector.tensor_copy(out=target[:, :VECTOR_SHARE, :, :], in_=source[:, :VECTOR_SHARE, :, :])
-            nc.scalar.copy(out=target[:, VECTOR_SHARE:, :, :], in_=source[:, VECTOR_SHARE:, :, :])
+            share = FIRST_SHARE if b == 0 and piece < PASSES else PARTS
+            nc.vector.tensor_copy(out=target[:, :share, :, :], in_=source[:, :share, :, :])
+            if share < PARTS:
+                nc.scalar.copy(out=target[:, share:, :, :], in_=source[:, share:, :, :])
             held[("grouped", b, piece)] = grouped
 
         def quantise_x(b, piece):
@@ -108,29 +110,20 @@ def tile_selfprojection_pb_kernel(
                 in_=held[("grouped", b, piece)][:].rearrange("p tn q tm -> p (tn q tm)"),
             )
 
+        def prepare(step):
+            if step < BATCH * PIECES:
+                regroup_x(step // PIECES, step % PIECES)
+            if step < PIECES:
+                quantise_x(0, step)
+            elif step > PIECES:
+                quantise_x((step - 1) // PIECES, (step - 1) % PIECES)
+
         def first_product_unit(b, unit):
             gn, jt = divmod(unit, TILES)
             x_codes = held[("x_codes", b)]
             x_planes = held[("x_planes", b)]
             if unit == 0:
                 held[("y_grouped", b)] = y_pool.tile([PARTS, PASSES, WIDTH, PACK], BF16, name="y_grouped", align_bytes=64)
-                held[("c_bank", b)] = psum_c.tile([PARTS, WIDTH], F32, name="c_bank")
-            c_bank = held[("c_bank", b)]
-            n_cols = slice(PARTS * unit, PARTS * (unit + 1))
-            for gm in range(PASSES):
-                nc.tensor.matmul_mx(
-                    out=c_bank[:],
-                    lhsT=x_codes[:, gm, n_cols].bitcast(FP8X4),
-                    lhsT_scale=x_planes[:, gm, n_cols],
-                    rhs=wj_codes[:, gm, :].bitcast(FP8X4),
-                    rhs_scale=wj_planes[:, gm, :],
-                    start=(unit == 0 and gm == 0),
-                    stop=(unit == UNITS - 1 and gm == PASSES - 1),
-                )
-            if unit == UNITS - 1:
-                c_parts = small.tile([PARTS, WIDTH], F32, name="c_parts")
-                nc.scalar.copy(out=c_parts[:], in_=c_bank[:])
-                held[("c_parts", b)] = c_parts
             j_cols = slice(PARTS * jt, PARTS * (jt + 1))
             y_bank = psum_y.tile([PARTS, PACK, PARTS], F32, name="y_bank")
             for tn in range(PACK):
@@ -157,53 +150,78 @@ def tile_selfprojection_pb_kernel(
                 in_=held[("y_grouped", b)][:, gn, :, :].rearrange("p j t -> p (j t)"),
             )
 
-        def collect_column_sum(b):
-            nc.tensor.matmul(
-                out=c_all[:], lhsT=pick[:, b, :], rhs=held[("c_parts", b)][:], start=(b == 0), stop=(b == BATCH - 1)
+        def column_sums(b, jt):
+            x_codes = held[("x_codes", b)]
+            x_planes = held[("x_planes", b)]
+            half = jt % HALVES
+            if half == 0:
+                held[("c_bank", b)] = psum_c.tile([PARTS, HALVES, C_WINDOW], F32, name="c_bank")
+            c_bank = held[("c_bank", b)]
+            j_cols = slice(PARTS * jt, PARTS * (jt + 1))
+            windows = N_COLS // C_WINDOW
+            for gm in range(PASSES):
+                for w in range(windows):
+                    n_cols = slice(C_WINDOW * w, C_WINDOW * (w + 1))
+                    nc.tensor.matmul_mx(
+                        out=c_bank[:, half, :],
+                        lhsT=wj_codes[:, gm, j_cols].bitcast(FP8X4),
+                        lhsT_scale=wj_planes[:, gm, j_cols],
+                        rhs=x_codes[:, gm, n_cols].bitcast(FP8X4),
+                        rhs_scale=x_planes[:, gm, n_cols],
+                        start=(gm == 0 and w == 0),
+                        stop=(gm == PASSES - 1 and w == windows - 1),
+                    )
+
+        def collect_sums(b, jt):
+            c_bank = held[("c_bank", b)]
+            for half in range(HALVES):
+                unused = s_pool.tile([PARTS, C_WINDOW], BF16, name="unused")
+                at = jt - HALVES + 1 + half
+                nc.scalar.activation(
+                    out=unused[:], in_=c_bank[:, half, :], func=ACT.Copy, accum_out=c_all[:, b, at : at + 1]
+                )
+
+        def second_product(b, it):
+            if it == 0:
+                held[("z_sb", b)] = z_pool.tile([PARTS, TILES, WIDTH], F32, name="z_sb")
+                held[("z_sum", b)] = small.tile([PARTS, TILES], F32, name="z_sum")
+            i_cols = slice(PARTS * it, PARTS * (it + 1))
+            z_bank = psum_z.tile([PARTS, WIDTH], F32, name="z_bank")
+            for gn in range(PASSES):
+                nc.tensor.matmul_mx(
+                    out=z_bank[:],
+                    lhsT=wi_codes[:, gn, i_cols].bitcast(FP8X4),
+                    lhsT_scale=wi_planes[:, gn, i_cols],
+                    rhs=held[("y_codes", b)][:, gn, :].bitcast(FP8X4),
+                    rhs_scale=held[("y_planes", b)][:, gn, :],
+                    start=(gn == 0),
+                    stop=(gn == PASSES - 1),
+                )
+            nc.scalar.activation(
+                out=held[("z_sb", b)][:, it, :], in_=z_bank[:], func=ACT.Copy, accum_out=held[("z_sum", b)][:, it : it + 1]
             )
 
-        def second_product(b):
-            z_sb = z_pool.tile([PARTS, TILES, WIDTH], F32, name="z_sb")
-            z_sum = small.tile([PARTS, TILES], F32, name="z_sum")
-            for it in range(TILES):
-                i_cols = slice(PARTS * it, PARTS * (it + 1))
-                z_bank = psum_z.tile([PARTS, WIDTH], F32, name="z_bank")
-                for gn in range(PASSES):
-                    nc.tensor.matmul_mx(
-                        out=z_bank[:],
-                        lhsT=wi_codes[:, gn, i_cols].bitcast(FP8X4),
-                        lhsT_scale=wi_planes[:, gn, i_cols],
-                        rhs=held[("y_codes", b)][:, gn, :].bitcast(FP8X4),
-                        rhs_scale=held[("y_planes", b)][:, gn, :],
-                        start=(gn == 0),
-                        stop=(gn == PASSES - 1),
-                    )
-                nc.scalar.activation(out=z_sb[:, it, :], in_=z_bank[:], func=ACT.Copy, accum_out=z_sum[:, it : it + 1])
-            held[("z_sb", b)] = z_sb
-            held[("z_sum", b)] = z_sum
-
-        def mean(b):
+        def mean_begin(b):
             mean_ps = psum_s.tile([PARTS, TILES], F32, name="mean_ps", tag="stat")
             nc.tensor.matmul(out=mean_ps[:], lhsT=neg_share[:], rhs=held[("z_sum", b)][:], start=True, stop=True)
+            held[("mean_ps", b)] = mean_ps
+
+        def mean_end(b):
             neg_mean = small.tile([PARTS, 1], F32, name="neg_mean")
-            nc.vector.tensor_reduce(out=neg_mean[:], in_=mean_ps[:], axis=AXIS.X, op=ALU.add)
+            nc.vector.tensor_reduce(out=neg_mean[:], in_=held[("mean_ps", b)][:], axis=AXIS.X, op=ALU.add)
             held[("neg_mean", b)] = neg_mean
-            held[("dev_sq", b)] = small.tile([PARTS, 1], F32, name="dev_sq")
-            held[("scaled", b)] = z_pool.tile([PARTS, TILES, WIDTH], F32, name="scaled")
 
         def deviations(b):
-            z_all = held[("z_sb", b)][:].rearrange("p t j -> p (t j)")
-            neg_mean = held[("neg_mean", b)]
-            squares = z_pool.tile([PARTS, TILES * WIDTH], BF16, name="squares")
-            nc.scalar.activation(out=squares[:], in_=z_all, func=ACT.Square, bias=neg_mean[:], accum_out=held[("dev_sq", b)][:])
-            nc.vector.scalar_tensor_tensor(
-                out=held[("scaled", b)][:].rearrange("p t j -> p (t j)"),
-                in0=z_all,
-                scalar=neg_mean[:],
-                in1=gamma_sb[:].rearrange("p t j -> p (t j)"),
-                op0=ALU.add,
-                op1=ALU.mult,
+            dev_sq = small.tile([PARTS, 1], F32, name="dev_sq")
+            squares = s_pool.tile([PARTS, TILES * WIDTH], BF16, name="squares")
+            nc.scalar.activation(
+                out=squares[:],
+                in_=held[("z_sb", b)][:].rearrange("p t j -> p (t j)"),
+                func=ACT.Square,
+                bias=held[("neg_mean", b)][:],
+                accum_out=dev_sq[:],
             )
+            held[("dev_sq", b)] = dev_sq
 
         def spread_begin(b):
             ssq_ps = psum_s.tile([PARTS, 1], F32, name="ssq_ps", tag="stat")
@@ -218,30 +236,90 @@ def tile_selfprojection_pb_kernel(
             nc.vector.reciprocal(out=inv_std[:], in_=inv_std[:])
             held[("inv_std", b)] = inv_std
 
-        def finish(b, it):
-            tile_out = held[("scaled", b)][:, it, :]
+        def scale_z(b, first, count):
+            if first == 0:
+                held[("scaled", b)] = s_pool.tile([PARTS, TILES, WIDTH], F32, name="scaled")
+            tiles = slice(first, first + count)
             nc.vector.scalar_tensor_tensor(
-                out=tile_out, in0=tile_out, scalar=held[("inv_std", b)][:], in1=beta_sb[:, it, :], op0=ALU.mult, op1=ALU.add
+                out=held[("scaled", b)][:, tiles, :],
+                in0=held[("z_sb", b)][:, tiles, :],
+                scalar=held[("neg_mean", b)][:],
+                in1=gamma_sb[:, tiles, :],
+                op0=ALU.add,
+                op1=ALU.mult,
             )
-            nc.sync.dma_start(out=out_0[b, PARTS * it : PARTS * (it + 1), :], in_=tile_out)
 
-        def normalise_column_sums():
-            c_stats = small.tile([BATCH, 6], F32, name="c_stats")
-            nc.vector.bn_stats(out=c_stats[:], in_=c_all[:BATCH, :])
-            c_mv = small.tile([BATCH, 2], F32, name="c_mv")
-            nc.vector.bn_aggr(out=c_mv[:], in_=c_stats[:])
-            c_std = small.tile([BATCH, 1], F32, name="c_std")
-            nc.scalar.activation(out=c_std[:], in_=c_mv[:, 1:2], func=ACT.Sqrt, scale=WIDTH / (WIDTH - 1.0))
-            c_inv = small.tile([BATCH, 1], F32, name="c_inv")
+        def finish(b, first, count):
+            tiles = slice(first, first + count)
+            part = held[("scaled", b)][:, tiles, :]
+            nc.vector.scalar_tensor_tensor(
+                out=part, in0=part, scalar=held[("inv_std", b)][:], in1=beta_sb[:, tiles, :], op0=ALU.mult, op1=ALU.add
+            )
+            nc.sync.dma_start(
+                out=out_0[b, PARTS * first : PARTS * (first + count), :].rearrange("(t p) j -> p t j", p=PARTS), in_=part
+            )
+
+        def centre_sums():
+            sums_ps = psum_s.tile([PARTS, BATCH, TILES], F32, name="sums_ps", tag="stat")
+            nc.tensor.matmul(
+                out=sums_ps[:].rearrange("p b t -> p (b t)"),
+                lhsT=ones[:],
+                rhs=c_all[:].rearrange("p b t -> p (b t)"),
+                start=True,
+                stop=True,
+            )
+            c_total = small.tile([PARTS, BATCH], F32, name="c_total")
+            nc.vector.tensor_reduce(out=c_total[:], in_=sums_ps[:], axis=AXIS.X, op=ALU.add)
+            c_dev = small.tile([PARTS, BATCH, TILES], F32, name="c_dev")
+            nc.vector.scalar_tensor_tensor(
+                out=c_dev[:],
+                in0=c_total[:].unsqueeze(2).to_broadcast([PARTS, BATCH, TILES]),
+                scalar=-1.0 / WIDTH,
+                in1=c_all[:],
+                op0=ALU.mult,
+                op1=ALU.add,
+            )
+            c_sq = small.tile([PARTS, BATCH, TILES], F32, name="c_sq")
+            nc.vector.tensor_mul(out=c_sq[:], in0=c_dev[:], in1=c_dev[:])
+            held["c_dev"] = c_dev
+            held["c_sq"] = c_sq
+
+        def spread_sums():
+            squares_ps = psum_s.tile([PARTS, BATCH, TILES], F32, name="squares_ps", tag="stat")
+            nc.tensor.matmul(
+                out=squares_ps[:].rearrange("p b t -> p (b t)"),
+                lhsT=ones[:],
+                rhs=held["c_sq"][:].rearrange("p b t -> p (b t)"),
+                start=True,
+                stop=True,
+            )
+            c_ssq = small.tile([PARTS, BATCH], F32, name="c_ssq")
+            nc.vector.tensor_reduce(out=c_ssq[:], in_=squares_ps[:], axis=AXIS.X, op=ALU.add)
+            c_std = small.tile([PARTS, BATCH], F32, name="c_std")
+            nc.scalar.activation(out=c_std[:], in_=c_ssq[:], func=ACT.Sqrt, scale=1.0 / (WIDTH - 1))
+            c_inv = small.tile([PARTS, BATCH], F32, name="c_inv")
             nc.vector.tensor_scalar_add(out=c_inv[:], in0=c_std[:], scalar1=EPS)
             nc.vector.reciprocal(out=c_inv[:], in_=c_inv[:])
-            p_sum = small.tile([BATCH, WIDTH], F32, name="p_sum")
-            nc.vector.tensor_scalar(
-                out=p_sum[:], in0=c_all[:BATCH, :], scalar1=c_mv[:, 0:1], scalar2=c_inv[:], op0=ALU.subtract, op1=ALU.mult
+            held["c_inv"] = c_inv
+
+        def store_sums():
+            shape = [PARTS, BATCH, TILES]
+            p_sum = held["c_dev"]
+            nc.vector.tensor_mul(out=p_sum[:], in0=p_sum[:], in1=held["c_inv"][:].unsqueeze(2).to_broadcast(shape))
+            nc.vector.tensor_mul(out=p_sum[:], in0=p_sum[:], in1=gain_c[:].unsqueeze(1).to_broadcast(shape))
+            nc.vector.scalar_tensor_tensor(
+                out=p_wide[:, : BATCH * TILES].rearrange("p (b t) -> p b t", t=TILES),
+                in0=p_sum[:],
+                scalar=1.0,
+                in1=bias_c[:].unsqueeze(1).to_broadcast(shape),
+                op0=ALU.add,
+                op1=ALU.add,
             )
-            nc.vector.tensor_mul(out=p_sum[:], in0=p_sum[:], in1=gain_c[:])
-            nc.vector.scalar_tensor_tensor(out=p_sum[:], in0=p_sum[:], scalar=1.0, in1=bias_c[:], op0=ALU.add, op1=ALU.add)
-            nc.sync.dma_start(out=out_1[:, :], in_=p_sum[:])
+            turned_ps = psum_s.tile([PARTS, PARTS], F32, name="turned_ps", tag="stat")
+            nc.tensor.transpose(turned_ps[:], p_wide[:], identity[:])
+            rows = small.tile([32, PARTS], F32, name="rows")
+            nc.scalar.copy(out=rows[:], in_=turned_ps[:32, :])
+            nc.sync.dma_start(out=out_1.rearrange("b (t j) -> (b t) j", j=PARTS), in_=rows[: BATCH * TILES, :])
 
         warm = keep.tile([PARTS, 1], F32, name="warm")
         nc.vector.memset(warm[:], 1.0)
@@ -250,56 +328,107 @@ def tile_selfprojection_pb_kernel(
         load_x(0, 0)
         wj_codes, wj_planes = load_weight(nc, keep, permuted_xj_y_words, permuted_xj_y_scales, "wj")
         load_x(0, 1)
-        wi_codes, wi_planes = load_weight(nc, keep, permuted_xi_y_words, permuted_xi_y_scales, "wi")
         load_x(1, 0)
+        wi_codes, wi_planes = load_weight(nc, keep, permuted_xi_y_words, permuted_xi_y_scales, "wi")
         load_x(1, 1)
         gamma_sb = keep.tile([PARTS, TILES, WIDTH], BF16, name="gamma_sb")
         beta_sb = keep.tile([PARTS, TILES, WIDTH], BF16, name="beta_sb")
-        nc.sync.dma_start(out=gamma_sb[:], in_=gamma_p.rearrange("(t p) j -> p t j", p=PARTS))
-        nc.sync.dma_start(out=beta_sb[:], in_=beta_p.rearrange("(t p) j -> p t j", p=PARTS))
-        gain_c = keep.tile([BATCH, WIDTH], BF16, name="gain_c")
-        bias_c = keep.tile([BATCH, WIDTH], BF16, name="bias_c")
-        nc.sync.dma_start(out=gain_c[:], in_=gamma_p_sum.partition_broadcast(BATCH))
-        nc.sync.dma_start(out=bias_c[:], in_=beta_p_sum.partition_broadcast(BATCH))
+        gain_c = keep.tile([PARTS, TILES], BF16, name="gain_c")
+        bias_c = keep.tile([PARTS, TILES], BF16, name="bias_c")
+
+        def load_gains():
+            nc.sync.dma_start(out=gamma_sb[:], in_=gamma_p.rearrange("(t p) j -> p t j", p=PARTS))
+            nc.sync.dma_start(out=beta_sb[:], in_=beta_p.rearrange("(t p) j -> p t j", p=PARTS))
+            with nc.allow_non_contiguous_dma(reason="two vectors of 512 values, laid along the partitions"):
+                nc.sync.dma_start(out=gain_c[:], in_=gamma_p_sum.rearrange("(t p) -> p t", p=PARTS))
+                nc.sync.dma_start(out=bias_c[:], in_=beta_p_sum.rearrange("(t p) -> p t", p=PARTS))
 
         ones = keep.tile([PARTS, PARTS], F32, name="ones")
         nc.gpsimd.memset(ones[:], 1.0)
         neg_share = keep.tile([PARTS, PARTS], F32, name="neg_share")
         nc.gpsimd.memset(neg_share[:], -1.0 / (WIDTH * WIDTH))
-        pick = keep.tile([PARTS, BATCH, PARTS], F32, name="pick")
-        nc.gpsimd.memset(pick[:], 0.0)
-        for b in range(BATCH):
-            nc.gpsimd.memset(pick[:, b, b : b + 1], 1.0)
-        c_all = psum_p.tile([PARTS, WIDTH], F32, name="c_all")
+        identity = keep.tile([PARTS, PARTS], F32, name="identity")
+        make_identity(nc, identity[:])
+        p_wide = keep.tile([PARTS, PARTS], F32, name="p_wide")
+        nc.gpsimd.memset(p_wide[:], 0.0)
+        c_all = keep.tile([PARTS, BATCH, TILES], F32, name="c_all")
 
-        for r in range(-1, BATCH + 2):
-            if r >= 0 and live(r + 2):
-                load_x(r + 2, 0)
-                load_x(r + 2, 1)
-            for unit in range(UNITS):
-                if live(r + 1):
-                    if unit % 2 == 0:
-                        regroup_x(r + 1, unit // 2)
+        ctx.enter_context(tc.manual_schedule(engines={mybir.EngineType.PE, mybir.EngineType.Activation, mybir.EngineType.DVE}))
+        made = {"steps": 0}
+
+        def prepare_to(steps):
+            for step in range(made["steps"], min(steps, BATCH * PIECES + 1)):
+                prepare(step)
+            made["steps"] = max(made["steps"], steps)
+
+        prepare_to(PASSES)
+        units = [("unit", i) for i in range(UNITS)]
+        sums = [("sum", i) for i in range(TILES)]
+        products = [("product", i) for i in range(TILES)]
+        for b in range(BATCH):
+            if b + 2 < BATCH:
+                load_x(b + 2, 0)
+                load_x(b + 2, 1)
+            if b == 0:
+                load_gains()
+            last = b == BATCH - 1
+            slots = units + sums + products if not last else units + sums[:HALVES] + products + sums[HALVES:]
+            begun = made["steps"]
+            closing = [] if b < 2 else [b - 2] if not last else [b - 2, b - 1]
+            finishing = [(i, part, first) for i in closing for part in range(2) for first in range(0, TILES, 2)]
+            n = len(finishing)
+            for slot, (kind, i) in enumerate(slots):
+                if kind == "unit":
+                    first_product_unit(b, i)
+                elif kind == "sum":
+                    column_sums(b, i)
+                    if i % HALVES == HALVES - 1 and not (last and i == TILES - 1):
+                        collect_sums(b, i)
+                else:
+                    second_product(b, i)
+                if b >= 1:
+                    if (kind, i) == ("unit", 1):
+                        mean_begin(b - 1)
+                    if (kind, i) == ("unit", 3):
+                        mean_end(b - 1)
+                    if (kind, i) == ("unit", UNITS - 1):
+                        deviations(b - 1)
+                    if (kind, i) == SPREAD_AFTER[last]:
+                        spread_begin(b - 1)
+                    if (kind, i) == SPREAD_END[last]:
+                        spread_end(b - 1)
+                if (kind, i) == ("unit", TILES):
+                    quantise_y(b, 0)
+                if (kind, i) == ("sum", 0):
+                    quantise_y(b, 1)
+                if b == 0 and slot < 2:
+                    prepare_to(PASSES + 1 + slot)
+                else:
+                    prepare_to(begun + (GOALS[b] - begun) * (slot + 1) // len(slots))
+                for item, part, first in finishing[n * slot // len(slots) : n * (slot + 1) // len(slots)]:
+                    if part == 0:
+                        scale_z(item, first, 2)
                     else:
-                        quantise_x(r + 1, unit // 2)
-                if live(r):
-                    first_product_unit(r, unit)
-                if live(r - 1) and unit == 1:
-                    collect_column_sum(r - 1)
-                    second_product(r - 1)
-                    if r - 1 == BATCH - 1:
-                        normalise_column_sums()
-                if live(r - 2):
-                    if unit == 1:
-                        spread_begin(r - 2)
-                    if unit == 2:
-                        spread_end(r - 2)
-                    if 2 <= unit < 2 + TILES:
-                        finish(r - 2, unit - 2)
-                if live(r - 1):
-                    if unit == TILES - 1:
-                        mean(r - 1)
-                    if unit == TILES:
-                        deviations(r - 1)
-                if live(r) and unit % TILES == TILES - 1:
-                    quantise_y(r, unit // TILES)
+                        finish(item, first, 2)
+                if last and (kind, i) == ("sum", HALVES):
+                    mean_begin(b)
+                    mean_end(b)
+                    deviations(b)
+        last = BATCH - 1
+        scale_z(last, 0, 2)
+        scale_z(last, 2, 2)
+        spread_begin(last)
+        collect_sums(last, TILES - 1)
+        spread_end(last)
+        finish(last, 0, 1)
+        centre_sums()
+        finish(last, 1, 1)
+        spread_sums()
+        finish(last, 2, 1)
+        finish(last, 3, 1)
+        store_sums()
+
+
+GOALS = [10, 16, 20, 23, 25, 25]
+SPREAD_AFTER = {False: ("sum", 2), True: ("product", 1)}
+SPREAD_END = {False: ("product", 0), True: ("product", 3)}

@@ -64,9 +64,9 @@ def tile_selfprojection_pb_kernel(
     nc = tc.nc
     with ExitStack() as ctx:
         keep = ctx.enter_context(tc.tile_pool(name="keep", bufs=1))
-        raw_pool = ctx.enter_context(tc.tile_pool(name="raw", bufs=3 * PIECES))
-        grouped_pool = ctx.enter_context(tc.tile_pool(name="grouped", bufs=3))
-        x_pool = ctx.enter_context(tc.tile_pool(name="xq", bufs=3))
+        raw_pool = ctx.enter_context(tc.tile_pool(name="raw", bufs=4 * PASSES))
+        grouped_pool = ctx.enter_context(tc.tile_pool(name="grouped", bufs=2))
+        x_pool = ctx.enter_context(tc.tile_pool(name="xq", bufs=2))
         y_pool = ctx.enter_context(tc.tile_pool(name="yq", bufs=2))
         z_pool = ctx.enter_context(tc.tile_pool(name="z", bufs=3))
         s_pool = ctx.enter_context(tc.tile_pool(name="s", bufs=2))
@@ -78,45 +78,37 @@ def tile_selfprojection_pb_kernel(
         held = {}
 
         def load_x(b, gn):
+            raw = raw_pool.tile([PARTS, PASSES, PACK, K_PASS], BF16, name="raw")
             for gm in range(PASSES):
-                piece = raw_pool.tile([PARTS, PACK, K_PASS], BF16, name="raw_piece")
                 nc.sync.dma_start(
-                    out=piece[:],
+                    out=raw[:, gm, :, :],
                     in_=x[b, K_PASS * gm : K_PASS * (gm + 1), K_PASS * gn : K_PASS * (gn + 1)].rearrange(
                         "(p t) n -> p t n", t=PACK
                     ),
                 )
-                held[("raw", b, PASSES * gn + gm)] = piece
+            held[("raw", b, gn)] = raw
 
-        def regroup_x(b, piece):
-            if piece == 0:
-                held[("x_codes", b)] = x_pool.tile([PARTS, PASSES, N_COLS], U32, name="x_codes", align_bytes=64)
-                held[("x_planes", b)] = x_pool.tile([PARTS, PASSES, N_COLS], U8, name="x_planes", align_bytes=64)
-            grouped = grouped_pool.tile([PARTS, PACK, PARTS, PACK], BF16, name="grouped", align_bytes=64)
-            source = held[("raw", b, piece)][:].rearrange("p tm (q tn) -> p q tm tn", tn=PACK)
-            target = grouped[:].rearrange("p tn q tm -> p q tm tn")
-            share = FIRST_SHARE if b == 0 and piece < PASSES else PARTS
+        def regroup_x(b, gn, gms):
+            if gn == 0 and gms.start == 0:
+                held[("x_codes", b)] = x_pool.tile([PARTS, PASSES, PASSES, K_PASS], U32, name="x_codes", align_bytes=64)
+                held[("x_planes", b)] = x_pool.tile([PARTS, PASSES, PASSES, K_PASS], U8, name="x_planes", align_bytes=64)
+            if gms.start == 0:
+                held[("grouped", b, gn)] = grouped_pool.tile(
+                    [PARTS, PASSES, PACK, PARTS, PACK], BF16, name="grouped", align_bytes=64
+                )
+            source = held[("raw", b, gn)][:, gms.start, :, :].rearrange("p tm (q tn) -> p q tm tn", tn=PACK)
+            target = held[("grouped", b, gn)][:, gms.start, :, :, :].rearrange("p tn q tm -> p q tm tn")
+            share = FIRST_SHARE if b == 0 and gn == 0 else PARTS
             nc.vector.tensor_copy(out=target[:, :share, :, :], in_=source[:, :share, :, :])
             if share < PARTS:
                 nc.scalar.copy(out=target[:, share:, :, :], in_=source[:, share:, :, :])
-            held[("grouped", b, piece)] = grouped
 
-        def quantise_x(b, piece):
-            gn, gm = divmod(piece, PASSES)
-            cols = slice(K_PASS * gn, K_PASS * (gn + 1))
+        def quantise_x(b, gn, gms):
             nc.vector.quantize_mx(
-                out=held[("x_codes", b)][:, gm, cols].bitcast(FP8X4),
-                scales=held[("x_planes", b)][:, gm, cols],
-                in_=held[("grouped", b, piece)][:].rearrange("p tn q tm -> p (tn q tm)"),
+                out=held[("x_codes", b)][:, gn, gms, :].rearrange("p gm n -> p (gm n)").bitcast(FP8X4),
+                scales=held[("x_planes", b)][:, gn, gms, :].rearrange("p gm n -> p (gm n)"),
+                in_=held[("grouped", b, gn)][:, gms, :, :, :].rearrange("p gm tn q tm -> p (gm tn q tm)"),
             )
-
-        def prepare(step):
-            if step < BATCH * PIECES:
-                regroup_x(step // PIECES, step % PIECES)
-            if step < PIECES:
-                quantise_x(0, step)
-            elif step > PIECES:
-                quantise_x((step - 1) // PIECES, (step - 1) % PIECES)
 
         def first_product_unit(b, unit):
             gn, jt = divmod(unit, TILES)
@@ -127,12 +119,12 @@ def tile_selfprojection_pb_kernel(
             j_cols = slice(PARTS * jt, PARTS * (jt + 1))
             y_bank = psum_y.tile([PARTS, PACK, PARTS], F32, name="y_bank")
             for tn in range(PACK):
-                n_cols = slice(K_PASS * gn + PARTS * tn, K_PASS * gn + PARTS * (tn + 1))
+                n_cols = slice(PARTS * tn, PARTS * (tn + 1))
                 for gm in range(PASSES):
                     nc.tensor.matmul_mx(
                         out=y_bank[:, tn, :],
-                        lhsT=x_codes[:, gm, n_cols].bitcast(FP8X4),
-                        lhsT_scale=x_planes[:, gm, n_cols],
+                        lhsT=x_codes[:, gn, gm, n_cols].bitcast(FP8X4),
+                        lhsT_scale=x_planes[:, gn, gm, n_cols],
                         rhs=wj_codes[:, gm, j_cols].bitcast(FP8X4),
                         rhs_scale=wj_planes[:, gm, j_cols],
                         start=(gm == 0),
@@ -158,18 +150,17 @@ def tile_selfprojection_pb_kernel(
                 held[("c_bank", b)] = psum_c.tile([PARTS, HALVES, C_WINDOW], F32, name="c_bank")
             c_bank = held[("c_bank", b)]
             j_cols = slice(PARTS * jt, PARTS * (jt + 1))
-            windows = N_COLS // C_WINDOW
+            windows = [(gn, slice(at, at + C_WINDOW)) for gn in range(PASSES) for at in range(0, K_PASS, C_WINDOW)]
             for gm in range(PASSES):
-                for w in range(windows):
-                    n_cols = slice(C_WINDOW * w, C_WINDOW * (w + 1))
+                for w, (gn, n_cols) in enumerate(windows):
                     nc.tensor.matmul_mx(
                         out=c_bank[:, half, :],
                         lhsT=wj_codes[:, gm, j_cols].bitcast(FP8X4),
                         lhsT_scale=wj_planes[:, gm, j_cols],
-                        rhs=x_codes[:, gm, n_cols].bitcast(FP8X4),
-                        rhs_scale=x_planes[:, gm, n_cols],
+                        rhs=x_codes[:, gn, gm, n_cols].bitcast(FP8X4),
+                        rhs_scale=x_planes[:, gn, gm, n_cols],
                         start=(gm == 0 and w == 0),
-                        stop=(gm == PASSES - 1 and w == windows - 1),
+                        stop=(gm == PASSES - 1 and w == len(windows) - 1),
                     )
 
         def collect_sums(b, jt):
@@ -228,12 +219,12 @@ def tile_selfprojection_pb_kernel(
             nc.tensor.matmul(out=ssq_ps[:], lhsT=ones[:], rhs=held[("dev_sq", b)][:], start=True, stop=True)
             std = small.tile([PARTS, 1], F32, name="std")
             nc.scalar.activation(out=std[:], in_=ssq_ps[:], func=ACT.Sqrt, scale=1.0 / (WIDTH * WIDTH - 1))
+            nc.scalar.activation(out=std[:], in_=std[:], func=ACT.Copy, bias=EPS)
             held[("std", b)] = std
 
         def spread_end(b):
             inv_std = small.tile([PARTS, 1], F32, name="inv_std")
-            nc.vector.tensor_scalar_add(out=inv_std[:], in0=held[("std", b)][:], scalar1=EPS)
-            nc.vector.reciprocal(out=inv_std[:], in_=inv_std[:])
+            nc.vector.reciprocal(out=inv_std[:], in_=held[("std", b)][:])
             held[("inv_std", b)] = inv_std
 
         def scale_z(b, first, count):
@@ -353,82 +344,62 @@ def tile_selfprojection_pb_kernel(
         nc.gpsimd.memset(p_wide[:], 0.0)
         c_all = keep.tile([PARTS, BATCH, TILES], F32, name="c_all")
 
-        ctx.enter_context(tc.manual_schedule(engines={mybir.EngineType.PE, mybir.EngineType.Activation, mybir.EngineType.DVE}))
-        made = {"steps": 0}
 
-        def prepare_to(steps):
-            for step in range(made["steps"], min(steps, BATCH * PIECES + 1)):
-                prepare(step)
-            made["steps"] = max(made["steps"], steps)
-
-        prepare_to(PASSES)
-        units = [("unit", i) for i in range(UNITS)]
-        sums = [("sum", i) for i in range(TILES)]
-        products = [("product", i) for i in range(TILES)]
+        whole = slice(0, PASSES)
+        for gn in range(PASSES):
+            for gm in range(PASSES):
+                regroup_x(0, gn, slice(gm, gm + 1))
+                quantise_x(0, gn, slice(gm, gm + 1))
+            for jt in range(TILES):
+                first_product_unit(0, TILES * gn + jt)
         for b in range(BATCH):
+            more = b + 1 < BATCH
             if b + 2 < BATCH:
                 load_x(b + 2, 0)
                 load_x(b + 2, 1)
             if b == 0:
                 load_gains()
-            last = b == BATCH - 1
-            slots = units + sums + products if not last else units + sums[:HALVES] + products + sums[HALVES:]
-            begun = made["steps"]
-            closing = [] if b < 2 else [b - 2] if not last else [b - 2, b - 1]
-            finishing = [(i, part, first) for i in closing for part in range(2) for first in range(0, TILES, 2)]
-            n = len(finishing)
-            for slot, (kind, i) in enumerate(slots):
-                if kind == "unit":
-                    first_product_unit(b, i)
-                elif kind == "sum":
-                    column_sums(b, i)
-                    if i % HALVES == HALVES - 1 and not (last and i == TILES - 1):
-                        collect_sums(b, i)
-                else:
-                    second_product(b, i)
-                if b >= 1:
-                    if (kind, i) == ("unit", 1):
-                        mean_begin(b - 1)
-                    if (kind, i) == ("unit", 3):
-                        mean_end(b - 1)
-                    if (kind, i) == ("unit", UNITS - 1):
-                        deviations(b - 1)
-                    if (kind, i) == SPREAD_AFTER[last]:
-                        spread_begin(b - 1)
-                    if (kind, i) == SPREAD_END[last]:
-                        spread_end(b - 1)
-                if (kind, i) == ("unit", TILES):
-                    quantise_y(b, 0)
-                if (kind, i) == ("sum", 0):
-                    quantise_y(b, 1)
-                if b == 0 and slot < 2:
-                    prepare_to(PASSES + 1 + slot)
-                else:
-                    prepare_to(begun + (GOALS[b] - begun) * (slot + 1) // len(slots))
-                for item, part, first in finishing[n * slot // len(slots) : n * (slot + 1) // len(slots)]:
-                    if part == 0:
-                        scale_z(item, first, 2)
-                    else:
-                        finish(item, first, 2)
-                if last and (kind, i) == ("sum", HALVES):
-                    mean_begin(b)
-                    mean_end(b)
-                    deviations(b)
+            if b >= 1:
+                mean_end(b - 1)
+                deviations(b - 1)
+            if more:
+                for gm in range(PASSES):
+                    regroup_x(b + 1, 0, slice(gm, gm + 1))
+            quantise_y(b, 0)
+            quantise_y(b, 1)
+            for jt in range(TILES):
+                column_sums(b, jt)
+                if jt % HALVES == HALVES - 1:
+                    collect_sums(b, jt)
+            if b >= 1:
+                spread_begin(b - 1)
+            if more:
+                for gm in range(PASSES):
+                    regroup_x(b + 1, 1, slice(gm, gm + 1))
+                quantise_x(b + 1, 0, whole)
+                quantise_x(b + 1, 1, whole)
+            for it in range(TILES):
+                second_product(b, it)
+            if b >= 1:
+                scale_z(b - 1, 0, TILES)
+            if more:
+                for unit in range(UNITS):
+                    first_product_unit(b + 1, unit)
+                    if unit == 1:
+                        mean_begin(b)
+            if b >= 1:
+                spread_end(b - 1)
+                finish(b - 1, 0, TILES)
         last = BATCH - 1
+        centre_sums()
+        mean_begin(last)
+        mean_end(last)
+        spread_sums()
+        deviations(last)
         scale_z(last, 0, 2)
         scale_z(last, 2, 2)
         spread_begin(last)
-        collect_sums(last, TILES - 1)
         spread_end(last)
-        finish(last, 0, 1)
-        centre_sums()
-        finish(last, 1, 1)
-        spread_sums()
-        finish(last, 2, 1)
-        finish(last, 3, 1)
+        for it in range(TILES):
+            finish(last, it, 1)
         store_sums()
-
-
-GOALS = [10, 16, 20, 23, 25, 25]
-SPREAD_AFTER = {False: ("sum", 2), True: ("product", 1)}
-SPREAD_END = {False: ("product", 0), True: ("product", 3)}

@@ -77,31 +77,34 @@ def tile_selfprojection_pb_kernel(
         psum_s = ctx.enter_context(tc.psum_pool(name="psum_s", bufs=1))
         held = {}
 
-        def load_x(b, gn):
+        def load_x(b, gn, cuts=1):
             raw = raw_pool.tile([PARTS, PASSES, PACK, K_PASS], BF16, name="raw")
+            width = K_PASS // cuts
             for gm in range(PASSES):
-                nc.sync.dma_start(
-                    out=raw[:, gm, :, :],
-                    in_=x[b, K_PASS * gm : K_PASS * (gm + 1), K_PASS * gn : K_PASS * (gn + 1)].rearrange(
-                        "(p t) n -> p t n", t=PACK
-                    ),
-                )
+                for at in range(0, K_PASS, width):
+                    start = K_PASS * gn + at
+                    nc.sync.dma_start(
+                        out=raw[:, gm, :, at : at + width],
+                        in_=x[b, K_PASS * gm : K_PASS * (gm + 1), start : start + width].rearrange(
+                            "(p t) n -> p t n", t=PACK
+                        ),
+                    )
             held[("raw", b, gn)] = raw
 
-        def regroup_x(b, gn, gms):
-            if gn == 0 and gms.start == 0:
+        def regroup_x(b, gn, gms, first=0, stop=PARTS, share=PARTS):
+            if gn == 0 and gms.start == 0 and first == 0:
                 held[("x_codes", b)] = x_pool.tile([PARTS, PASSES, PASSES, K_PASS], U32, name="x_codes", align_bytes=64)
                 held[("x_planes", b)] = x_pool.tile([PARTS, PASSES, PASSES, K_PASS], U8, name="x_planes", align_bytes=64)
-            if gms.start == 0:
+            if gms.start == 0 and first == 0:
                 held[("grouped", b, gn)] = grouped_pool.tile(
                     [PARTS, PASSES, PACK, PARTS, PACK], BF16, name="grouped", align_bytes=64
                 )
             source = held[("raw", b, gn)][:, gms.start, :, :].rearrange("p tm (q tn) -> p q tm tn", tn=PACK)
             target = held[("grouped", b, gn)][:, gms.start, :, :, :].rearrange("p tn q tm -> p q tm tn")
-            share = FIRST_SHARE if b == 0 and gn == 0 else PARTS
-            nc.vector.tensor_copy(out=target[:, :share, :, :], in_=source[:, :share, :, :])
-            if share < PARTS:
-                nc.scalar.copy(out=target[:, share:, :, :], in_=source[:, share:, :, :])
+            cut = first + (stop - first) * share // PARTS
+            nc.vector.tensor_copy(out=target[:, first:cut, :, :], in_=source[:, first:cut, :, :])
+            if cut < stop:
+                nc.scalar.copy(out=target[:, cut:stop, :, :], in_=source[:, cut:stop, :, :])
 
         def quantise_x(b, gn, gms):
             nc.vector.quantize_mx(
@@ -316,7 +319,7 @@ def tile_selfprojection_pb_kernel(
         nc.vector.memset(warm[:], 1.0)
         nc.scalar.activation(out=warm[:], in_=warm[:], func=ACT.Sqrt)
 
-        load_x(0, 0)
+        load_x(0, 0, 1)
         wj_codes, wj_planes = load_weight(nc, keep, permuted_xj_y_words, permuted_xj_y_scales, "wj")
         load_x(0, 1)
         load_x(1, 0)
@@ -346,9 +349,16 @@ def tile_selfprojection_pb_kernel(
 
 
         whole = slice(0, PASSES)
+        def sum_columns(b):
+            for jt in range(TILES):
+                column_sums(b, jt)
+                if jt % HALVES == HALVES - 1:
+                    collect_sums(b, jt)
+
         for gn in range(PASSES):
             for gm in range(PASSES):
-                regroup_x(0, gn, slice(gm, gm + 1))
+                for at in range(0, PARTS, PARTS // (1 if gn == 0 else 1)):
+                    regroup_x(0, gn, slice(gm, gm + 1), at, at + PARTS // (1 if gn == 0 else 1), FIRST_SHARE if gn == 0 else 128)
                 quantise_x(0, gn, slice(gm, gm + 1))
             for jt in range(TILES):
                 first_product_unit(0, TILES * gn + jt)
@@ -364,22 +374,22 @@ def tile_selfprojection_pb_kernel(
                 deviations(b - 1)
             if more:
                 for gm in range(PASSES):
-                    regroup_x(b + 1, 0, slice(gm, gm + 1))
+                    regroup_x(b + 1, 0, slice(gm, gm + 1), share=SHARE1[b == 0])
             quantise_y(b, 0)
             quantise_y(b, 1)
-            for jt in range(TILES):
-                column_sums(b, jt)
-                if jt % HALVES == HALVES - 1:
-                    collect_sums(b, jt)
+            if not more:
+                sum_columns(b)
             if b >= 1:
                 spread_begin(b - 1)
             if more:
                 for gm in range(PASSES):
-                    regroup_x(b + 1, 1, slice(gm, gm + 1))
+                    regroup_x(b + 1, 1, slice(gm, gm + 1), share=SHARE1[b == 0])
                 quantise_x(b + 1, 0, whole)
                 quantise_x(b + 1, 1, whole)
             for it in range(TILES):
                 second_product(b, it)
+            if more:
+                sum_columns(b)
             if b >= 1:
                 scale_z(b - 1, 0, TILES)
             if more:
@@ -387,10 +397,12 @@ def tile_selfprojection_pb_kernel(
                     first_product_unit(b + 1, unit)
                     if unit == 1:
                         mean_begin(b)
-            if b >= 1:
-                spread_end(b - 1)
-                finish(b - 1, 0, TILES)
+            if b >= 2:
+                spread_end(b - 2)
+                finish(b - 2, 0, TILES)
         last = BATCH - 1
+        spread_end(last - 1)
+        finish(last - 1, 0, TILES)
         centre_sums()
         mean_begin(last)
         mean_end(last)
@@ -403,3 +415,6 @@ def tile_selfprojection_pb_kernel(
         for it in range(TILES):
             finish(last, it, 1)
         store_sums()
+
+
+SHARE1 = {True: 112, False: 120}

from contextlib import ExitStack

import concourse.mybir as mybir
from concourse.masks import make_identity

FP8X4 = mybir.dt.float8_e4m3fn_x4
BF16 = mybir.dt.bfloat16
F32 = mybir.dt.float32
U32 = mybir.dt.uint32
I32 = mybir.dt.int32
U8 = mybir.dt.uint8
ACT = mybir.ActivationFunctionType
ALU = mybir.AluOpType
AXIS = mybir.AxisListType

BATCH = 6
M_ROWS = 1024
N_COLS = 1024
WIDTH = 512
EPS = 1e-05

PARTS = 128
PACK = 4
K_PASS = PARTS * PACK
PASSES = M_ROWS // K_PASS
TILES = WIDTH // PARTS
SCALE_ROWS = K_PASS // 32
UNITS = PASSES * TILES
PIECES = PASSES * PASSES
C_WINDOW = 256
HALVES = 2
FIRST_SHARE = 88

FLOPS = 2 * BATCH * (M_ROWS * N_COLS * WIDTH + N_COLS * WIDTH * WIDTH)


def load_weight(nc, keep, words, scales, label):
    codes = keep.tile([PARTS, PASSES, WIDTH], U32, name=label + "_codes", align_bytes=64)
    planes = keep.tile([PARTS, PASSES, WIDTH], U8, name=label + "_planes", align_bytes=64)
    nc.vector.memset(planes[:].bitcast(I32), 0)
    nc.sync.dma_start(out=codes[:].bitcast(I32), in_=words.rearrange("g p n t -> p g (n t)").bitcast(I32))
    for r in range(PACK):
        nc.sync.dma_start(
            out=planes[r:PARTS:32, :, :].bitcast(I32),
            in_=scales[:, r:SCALE_ROWS:PACK, :].rearrange("g q n -> q g n").bitcast(I32),
        )
    return codes, planes


def tile_selfprojection_pb_kernel(
    tc,
    x,
    permuted_xj_y_words,
    permuted_xj_y_scales,
    permuted_xi_y_words,
    permuted_xi_y_scales,
    gamma_p_sum,
    gamma_p,
    beta_p_sum,
    beta_p,
    out_0,
    out_1,
):
    nc = tc.nc
    with ExitStack() as ctx:
        keep = ctx.enter_context(tc.tile_pool(name="keep", bufs=1))
        raw_pool = ctx.enter_context(tc.tile_pool(name="raw", bufs=4 * PASSES))
        grouped_pool = ctx.enter_context(tc.tile_pool(name="grouped", bufs=2))
        x_pool = ctx.enter_context(tc.tile_pool(name="xq", bufs=2))
        y_pool = ctx.enter_context(tc.tile_pool(name="yq", bufs=2))
        z_pool = ctx.enter_context(tc.tile_pool(name="z", bufs=3))
        s_pool = ctx.enter_context(tc.tile_pool(name="s", bufs=2))
        small = ctx.enter_context(tc.tile_pool(name="small", bufs=4))
        psum_y = ctx.enter_context(tc.psum_pool(name="psum_y", bufs=3))
        psum_c = ctx.enter_context(tc.psum_pool(name="psum_c", bufs=2))
        psum_z = ctx.enter_context(tc.psum_pool(name="psum_z", bufs=2))
        psum_s = ctx.enter_context(tc.psum_pool(name="psum_s", bufs=1))
        held = {}

        def load_x(b, gn, cuts=1):
            raw = raw_pool.tile([PARTS, PASSES, PACK, K_PASS], BF16, name="raw")
            width = K_PASS // cuts
            for gm in range(PASSES):
                for at in range(0, K_PASS, width):
                    start = K_PASS * gn + at
                    nc.sync.dma_start(
                        out=raw[:, gm, :, at : at + width],
                        in_=x[b, K_PASS * gm : K_PASS * (gm + 1), start : start + width].rearrange(
                            "(p t) n -> p t n", t=PACK
                        ),
                    )
            held[("raw", b, gn)] = raw

        def regroup_x(b, gn, gms, first=0, stop=PARTS, share=PARTS):
            if gn == 0 and gms.start == 0 and first == 0:
                held[("x_codes", b)] = x_pool.tile([PARTS, PASSES, PASSES, K_PASS], U32, name="x_codes", align_bytes=64)
                held[("x_planes", b)] = x_pool.tile([PARTS, PASSES, PASSES, K_PASS], U8, name="x_planes", align_bytes=64)
            if gms.start == 0 and first == 0:
                held[("grouped", b, gn)] = grouped_pool.tile(
                    [PARTS, PASSES, PACK, PARTS, PACK], BF16, name="grouped", align_bytes=64
                )
            source = held[("raw", b, gn)][:, gms.start, :, :].rearrange("p tm (q tn) -> p q tm tn", tn=PACK)
            target = held[("grouped", b, gn)][:, gms.start, :, :, :].rearrange("p tn q tm -> p q tm tn")
            cut = first + (stop - first) * share // PARTS
            nc.vector.tensor_copy(out=target[:, first:cut, :, :], in_=source[:, first:cut, :, :])
            if cut < stop:
                nc.scalar.copy(out=target[:, cut:stop, :, :], in_=source[:, cut:stop, :, :])

        def quantise_x(b, gn, gms):
            nc.vector.quantize_mx(
                out=held[("x_codes", b)][:, gn, gms, :].rearrange("p gm n -> p (gm n)").bitcast(FP8X4),
                scales=held[("x_planes", b)][:, gn, gms, :].rearrange("p gm n -> p (gm n)"),
                in_=held[("grouped", b, gn)][:, gms, :, :, :].rearrange("p gm tn q tm -> p (gm tn q tm)"),
            )

        def first_product_unit(b, unit):
            gn, jt = divmod(unit, TILES)
            x_codes = held[("x_codes", b)]
            x_planes = held[("x_planes", b)]
            if unit == 0:
                held[("y_grouped", b)] = y_pool.tile([PARTS, PASSES, WIDTH, PACK], BF16, name="y_grouped", align_bytes=64)
            j_cols = slice(PARTS * jt, PARTS * (jt + 1))
            y_bank = psum_y.tile([PARTS, PACK, PARTS], F32, name="y_bank")
            for tn in range(PACK):
                n_cols = slice(PARTS * tn, PARTS * (tn + 1))
                for gm in range(PASSES):
                    nc.tensor.matmul_mx(
                        out=y_bank[:, tn, :],
                        lhsT=x_codes[:, gn, gm, n_cols].bitcast(FP8X4),
                        lhsT_scale=x_planes[:, gn, gm, n_cols],
                        rhs=wj_codes[:, gm, j_cols].bitcast(FP8X4),
                        rhs_scale=wj_planes[:, gm, j_cols],
                        start=(gm == 0),
                        stop=(gm == PASSES - 1),
                    )
            nc.scalar.copy(out=held[("y_grouped", b)][:, gn, j_cols, :], in_=y_bank[:].rearrange("p t j -> p j t"))

        def quantise_y(b, gn):
            if gn == 0:
                held[("y_codes", b)] = y_pool.tile([PARTS, PASSES, WIDTH], U32, name="y_codes", align_bytes=64)
                held[("y_planes", b)] = y_pool.tile([PARTS, PASSES, WIDTH], U8, name="y_planes", align_bytes=64)
            nc.vector.quantize_mx(
                out=held[("y_codes", b)][:, gn, :].bitcast(FP8X4),
                scales=held[("y_planes", b)][:, gn, :],
                in_=held[("y_grouped", b)][:, gn, :, :].rearrange("p j t -> p (j t)"),
            )

        def column_sums(b, jt):
            x_codes = held[("x_codes", b)]
            x_planes = held[("x_planes", b)]
            half = jt % HALVES
            if half == 0:
                held[("c_bank", b)] = psum_c.tile([PARTS, HALVES, C_WINDOW], F32, name="c_bank")
            c_bank = held[("c_bank", b)]
            j_cols = slice(PARTS * jt, PARTS * (jt + 1))
            windows = [(gn, slice(at, at + C_WINDOW)) for gn in range(PASSES) for at in range(0, K_PASS, C_WINDOW)]
            for gm in range(PASSES):
                for w, (gn, n_cols) in enumerate(windows):
                    nc.tensor.matmul_mx(
                        out=c_bank[:, half, :],
                        lhsT=wj_codes[:, gm, j_cols].bitcast(FP8X4),
                        lhsT_scale=wj_planes[:, gm, j_cols],
                        rhs=x_codes[:, gn, gm, n_cols].bitcast(FP8X4),
                        rhs_scale=x_planes[:, gn, gm, n_cols],
                        start=(gm == 0 and w == 0),
                        stop=(gm == PASSES - 1 and w == len(windows) - 1),
                    )

        def collect_sums(b, jt):
            c_bank = held[("c_bank", b)]
            for half in range(HALVES):
                unused = s_pool.tile([PARTS, C_WINDOW], BF16, name="unused")
                at = jt - HALVES + 1 + half
                nc.scalar.activation(
                    out=unused[:], in_=c_bank[:, half, :], func=ACT.Copy, accum_out=c_all[:, b, at : at + 1]
                )

        def second_product(b, it):
            if it == 0:
                held[("z_sb", b)] = z_pool.tile([PARTS, TILES, WIDTH], F32, name="z_sb")
                held[("z_sum", b)] = small.tile([PARTS, TILES], F32, name="z_sum")
            i_cols = slice(PARTS * it, PARTS * (it + 1))
            z_bank = psum_z.tile([PARTS, WIDTH], F32, name="z_bank")
            for gn in range(PASSES):
                nc.tensor.matmul_mx(
                    out=z_bank[:],
                    lhsT=wi_codes[:, gn, i_cols].bitcast(FP8X4),
                    lhsT_scale=wi_planes[:, gn, i_cols],
                    rhs=held[("y_codes", b)][:, gn, :].bitcast(FP8X4),
                    rhs_scale=held[("y_planes", b)][:, gn, :],
                    start=(gn == 0),
                    stop=(gn == PASSES - 1),
                )
            nc.scalar.activation(
                out=held[("z_sb", b)][:, it, :], in_=z_bank[:], func=ACT.Copy, accum_out=held[("z_sum", b)][:, it : it + 1]
            )

        def mean_begin(b):
            mean_ps = psum_s.tile([PARTS, TILES], F32, name="mean_ps", tag="stat")
            nc.tensor.matmul(out=mean_ps[:], lhsT=neg_share[:], rhs=held[("z_sum", b)][:], start=True, stop=True)
            held[("mean_ps", b)] = mean_ps

        def mean_end(b):
            neg_mean = small.tile([PARTS, 1], F32, name="neg_mean")
            nc.vector.tensor_reduce(out=neg_mean[:], in_=held[("mean_ps", b)][:], axis=AXIS.X, op=ALU.add)
            held[("neg_mean", b)] = neg_mean

        def deviations(b):
            dev_sq = small.tile([PARTS, 1], F32, name="dev_sq")
            squares = s_pool.tile([PARTS, TILES * WIDTH], BF16, name="squares")
            nc.scalar.activation(
                out=squares[:],
                in_=held[("z_sb", b)][:].rearrange("p t j -> p (t j)"),
                func=ACT.Square,
                bias=held[("neg_mean", b)][:],
                accum_out=dev_sq[:],
            )
            held[("dev_sq", b)] = dev_sq

        def spread_begin(b):
            ssq_ps = psum_s.tile([PARTS, 1], F32, name="ssq_ps", tag="stat")
            nc.tensor.matmul(out=ssq_ps[:], lhsT=ones[:], rhs=held[("dev_sq", b)][:], start=True, stop=True)
            std = small.tile([PARTS, 1], F32, name="std")
            nc.scalar.activation(out=std[:], in_=ssq_ps[:], func=ACT.Sqrt, scale=1.0 / (WIDTH * WIDTH - 1))
            nc.scalar.activation(out=std[:], in_=std[:], func=ACT.Copy, bias=EPS)
            held[("std", b)] = std

        def spread_end(b):
            inv_std = small.tile([PARTS, 1], F32, name="inv_std")
            nc.vector.reciprocal(out=inv_std[:], in_=held[("std", b)][:])
            held[("inv_std", b)] = inv_std

        def scale_z(b, first, count):
            if first == 0:
                held[("scaled", b)] = s_pool.tile([PARTS, TILES, WIDTH], F32, name="scaled")
            tiles = slice(first, first + count)
            nc.vector.scalar_tensor_tensor(
                out=held[("scaled", b)][:, tiles, :],
                in0=held[("z_sb", b)][:, tiles, :],
                scalar=held[("neg_mean", b)][:],
                in1=gamma_sb[:, tiles, :],
                op0=ALU.add,
                op1=ALU.mult,
            )

        def finish(b, first, count):
            tiles = slice(first, first + count)
            part = held[("scaled", b)][:, tiles, :]
            nc.vector.scalar_tensor_tensor(
                out=part, in0=part, scalar=held[("inv_std", b)][:], in1=beta_sb[:, tiles, :], op0=ALU.mult, op1=ALU.add
            )
            nc.sync.dma_start(
                out=out_0[b, PARTS * first : PARTS * (first + count), :].rearrange("(t p) j -> p t j", p=PARTS), in_=part
            )

        def centre_sums():
            sums_ps = psum_s.tile([PARTS, BATCH, TILES], F32, name="sums_ps", tag="stat")
            nc.tensor.matmul(
                out=sums_ps[:].rearrange("p b t -> p (b t)"),
                lhsT=ones[:],
                rhs=c_all[:].rearrange("p b t -> p (b t)"),
                start=True,
                stop=True,
            )
            c_total = small.tile([PARTS, BATCH], F32, name="c_total")
            nc.vector.tensor_reduce(out=c_total[:], in_=sums_ps[:], axis=AXIS.X, op=ALU.add)
            c_dev = small.tile([PARTS, BATCH, TILES], F32, name="c_dev")
            nc.vector.scalar_tensor_tensor(
                out=c_dev[:],
                in0=c_total[:].unsqueeze(2).to_broadcast([PARTS, BATCH, TILES]),
                scalar=-1.0 / WIDTH,
                in1=c_all[:],
                op0=ALU.mult,
                op1=ALU.add,
            )
            c_sq = small.tile([PARTS, BATCH, TILES], F32, name="c_sq")
            nc.vector.tensor_mul(out=c_sq[:], in0=c_dev[:], in1=c_dev[:])
            held["c_dev"] = c_dev
            held["c_sq"] = c_sq

        def spread_sums():
            squares_ps = psum_s.tile([PARTS, BATCH, TILES], F32, name="squares_ps", tag="stat")
            nc.tensor.matmul(
                out=squares_ps[:].rearrange("p b t -> p (b t)"),
                lhsT=ones[:],
                rhs=held["c_sq"][:].rearrange("p b t -> p (b t)"),
                start=True,
                stop=True,
            )
            c_ssq = small.tile([PARTS, BATCH], F32, name="c_ssq")
            nc.vector.tensor_reduce(out=c_ssq[:], in_=squares_ps[:], axis=AXIS.X, op=ALU.add)
            c_std = small.tile([PARTS, BATCH], F32, name="c_std")
            nc.scalar.activation(out=c_std[:], in_=c_ssq[:], func=ACT.Sqrt, scale=1.0 / (WIDTH - 1))
            c_inv = small.tile([PARTS, BATCH], F32, name="c_inv")
            nc.vector.tensor_scalar_add(out=c_inv[:], in0=c_std[:], scalar1=EPS)
            nc.vector.reciprocal(out=c_inv[:], in_=c_inv[:])
            held["c_inv"] = c_inv

        def store_sums():
            shape = [PARTS, BATCH, TILES]
            p_sum = held["c_dev"]
            nc.vector.tensor_mul(out=p_sum[:], in0=p_sum[:], in1=held["c_inv"][:].unsqueeze(2).to_broadcast(shape))
            nc.vector.tensor_mul(out=p_sum[:], in0=p_sum[:], in1=gain_c[:].unsqueeze(1).to_broadcast(shape))
            nc.vector.scalar_tensor_tensor(
                out=p_wide[:, : BATCH * TILES].rearrange("p (b t) -> p b t", t=TILES),
                in0=p_sum[:],
                scalar=1.0,
                in1=bias_c[:].unsqueeze(1).to_broadcast(shape),
                op0=ALU.add,
                op1=ALU.add,
            )
            turned_ps = psum_s.tile([PARTS, PARTS], F32, name="turned_ps", tag="stat")
            nc.tensor.transpose(turned_ps[:], p_wide[:], identity[:])
            rows = small.tile([32, PARTS], F32, name="rows")
            nc.scalar.copy(out=rows[:], in_=turned_ps[:32, :])
            nc.sync.dma_start(out=out_1.rearrange("b (t j) -> (b t) j", j=PARTS), in_=rows[: BATCH * TILES, :])

        warm = keep.tile([PARTS, 1], F32, name="warm")
        nc.vector.memset(warm[:], 1.0)
        nc.scalar.activation(out=warm[:], in_=warm[:], func=ACT.Sqrt)

        load_x(0, 0, 1)
        wj_codes, wj_planes = load_weight(nc, keep, permuted_xj_y_words, permuted_xj_y_scales, "wj")
        load_x(0, 1)
        load_x(1, 0)
        wi_codes, wi_planes = load_weight(nc, keep, permuted_xi_y_words, permuted_xi_y_scales, "wi")
        load_x(1, 1)
        gamma_sb = keep.tile([PARTS, TILES, WIDTH], BF16, name="gamma_sb")
        beta_sb = keep.tile([PARTS, TILES, WIDTH], BF16, name="beta_sb")
        gain_c = keep.tile([PARTS, TILES], BF16, name="gain_c")
        bias_c = keep.tile([PARTS, TILES], BF16, name="bias_c")

        def load_gains():
            nc.sync.dma_start(out=gamma_sb[:], in_=gamma_p.rearrange("(t p) j -> p t j", p=PARTS))
            nc.sync.dma_start(out=beta_sb[:], in_=beta_p.rearrange("(t p) j -> p t j", p=PARTS))
            with nc.allow_non_contiguous_dma(reason="two vectors of 512 values, laid along the partitions"):
                nc.sync.dma_start(out=gain_c[:], in_=gamma_p_sum.rearrange("(t p) -> p t", p=PARTS))
                nc.sync.dma_start(out=bias_c[:], in_=beta_p_sum.rearrange("(t p) -> p t", p=PARTS))

        ones = keep.tile([PARTS, PARTS], F32, name="ones")
        nc.gpsimd.memset(ones[:], 1.0)
        neg_share = keep.tile([PARTS, PARTS], F32, name="neg_share")
        nc.gpsimd.memset(neg_share[:], -1.0 / (WIDTH * WIDTH))
        identity = keep.tile([PARTS, PARTS], F32, name="identity")
        make_identity(nc, identity[:])
        p_wide = keep.tile([PARTS, PARTS], F32, name="p_wide")
        nc.gpsimd.memset(p_wide[:], 0.0)
        c_all = keep.tile([PARTS, BATCH, TILES], F32, name="c_all")


        whole = slice(0, PASSES)
        def sum_columns(b):
            for jt in range(TILES):
                column_sums(b, jt)
                if jt % HALVES == HALVES - 1:
                    collect_sums(b, jt)

        for gn in range(PASSES):
            for gm in range(PASSES):
                for at in range(0, PARTS, PARTS // (1 if gn == 0 else 1)):
                    regroup_x(0, gn, slice(gm, gm + 1), at, at + PARTS // (1 if gn == 0 else 1), FIRST_SHARE if gn == 0 else 128)
                quantise_x(0, gn, slice(gm, gm + 1))
            for jt in range(TILES):
                first_product_unit(0, TILES * gn + jt)
        for b in range(BATCH):
            more = b + 1 < BATCH
            if b + 2 < BATCH:
                load_x(b + 2, 0)
                load_x(b + 2, 1)
            if b == 0:
                load_gains()
            if b >= 1:
                mean_end(b - 1)
                deviations(b - 1)
            if more:
                for gm in range(PASSES):
                    regroup_x(b + 1, 0, slice(gm, gm + 1), share=SHARE1[b == 0])
            quantise_y(b, 0)
            quantise_y(b, 1)
            if not more:
                sum_columns(b)
            if b >= 1:
                spread_begin(b - 1)
            if more:
                for gm in range(PASSES):
                    regroup_x(b + 1, 1, slice(gm, gm + 1), share=SHARE1[b == 0])
                quantise_x(b + 1, 0, whole)
                quantise_x(b + 1, 1, whole)
            for it in range(TILES):
                second_product(b, it)
            if more:
                sum_columns(b)
            if b >= 1:
                scale_z(b - 1, 0, TILES)
            if more:
                for unit in range(UNITS):
                    first_product_unit(b + 1, unit)
                    if unit == 1:
                        mean_begin(b)
            if b >= 2:
                spread_end(b - 2)
                finish(b - 2, 0, TILES)
        last = BATCH - 1
        spread_end(last - 1)
        finish(last - 1, 0, TILES)
        centre_sums()
        mean_begin(last)
        mean_end(last)
        spread_sums()
        deviations(last)
        scale_z(last, 0, 2)
        scale_z(last, 2, 2)
        spread_begin(last)
        spread_end(last)
        for it in range(TILES):
            finish(last, it, 1)
        store_sums()


SHARE1 = {True: 112, False: 120}
